import numpy as np
import ml_dtypes


def mxq(x, axis, fmt="e4m3"):
    dtype, down = {"e4m3": (ml_dtypes.float8_e4m3fn, 7), "e5m2": (ml_dtypes.float8_e5m2, 14)}[fmt]
    v = np.moveaxis(np.asarray(x, np.float32).astype(ml_dtypes.bfloat16).astype(np.float64), axis, -1)
    blocks = v.reshape(v.shape[:-1] + (-1, 32))
    amax = np.abs(blocks).max(-1, keepdims=True)
    byte = np.maximum(np.where(amax > 0, np.frexp(amax)[1] - 1 + 127, 0) - down, 1)
    scale = np.exp2(byte - 127.0)
    codes = (blocks / scale).astype(np.float32).astype(dtype).astype(np.float64)
    return np.moveaxis((codes * scale).reshape(v.shape), -1, axis)


WIDE = False


def mx_kscale(k):
    if not WIDE:
        return np.ones(k)
    levels = np.array([10, -10, 5, -5, 0])
    a = np.random.permutation(np.resize(levels, k // 512 * 4)).reshape(k // 512, 4)
    idx = np.arange(k)
    return np.exp2(a[idx // 512, idx % 128 // 32])


BF16 = ml_dtypes.bfloat16


def bf(x):
    return np.asarray(x, np.float32).astype(BF16)


def f64(x):
    return np.asarray(x).astype(np.float64)


B, E, D, H = 256, 8, 128, 1024
FACTOR = 1.0


def swish(v):
    return v / (1.0 + np.exp(-v))


def setup_inputs():
    s = mx_kscale(H)
    return {"h2": bf(swish(np.random.standard_normal((B, E, H)) * 1.5) * s),
            "W3": bf(np.random.standard_normal((E, H, H)) * 1.5 / np.sqrt(H) / s[:, None]),
            "b3": bf(np.random.standard_normal((E, H)) * 0.3),
            "W4": bf(np.random.standard_normal((E, H, D)) / np.sqrt(H)),
            "b4": bf(np.random.standard_normal((E, D)) * 0.3)}


def reference(h2, W3, b3, W4, b4):
    x = f64(h2).transpose(1, 0, 2)
    h3 = swish((mxq(x, 2, "e4m3") @ mxq(f64(W3), 1, "e4m3")) + f64(b3)[:, None, :])
    out = ((mxq(h3, 2, "e4m3") @ mxq(f64(W4), 1, "e4m3")) + f64(b4)[:, None, :]) * FACTOR
    return out.transpose(1, 0, 2).reshape(-1, D)

@@ -1,0 +1,187 @@
+from contextlib import ExitStack
+
+import concourse.mybir as mybir
+from concourse.masks import make_identity
+
+BF16 = mybir.dt.bfloat16
+F32 = mybir.dt.float32
+U32 = mybir.dt.uint32
+U8 = mybir.dt.uint8
+FP8X4 = mybir.dt.float8_e4m3fn_x4
+ACT = mybir.ActivationFunctionType
+ALU = mybir.AluOpType
+
+P = 128
+B, E, D, H = 256, 8, 128, 1024
+FLOPS = 2 * E * B * H * (H + D)
+
+
+def regroup_views(dst, src):
+    return (
+        dst.rearrange("p (c i t) -> p c t i", i=4, t=4),
+        src.rearrange("p t (c i) -> p c t i", i=4),
+    )
+
+
+def tile_environvectorfield_pb_kernel(tc, h2, W3, b3, W4, b4, out):
+    nc = tc.nc
+    h2v = h2.rearrange("(p bt) e k -> e p bt k", bt=2)
+    w3v = W3.rearrange("e (g u p r) n -> e g p u (r n)", g=2, u=2, p=P, r=2)
+    w4v = W4.rearrange("e (a p) d -> e p a d", p=P)
+    b3v = b3.rearrange("e (j q) -> (e j) q", q=P)
+    outv = out.rearrange("(p bt e) d -> e p bt d", bt=2, e=E)
+
+    with ExitStack() as ctx:
+        const = ctx.enter_context(tc.tile_pool(name="const", bufs=1))
+        rawp = ctx.enter_context(tc.tile_pool(name="rawp", bufs=8))
+        grpp = ctx.enter_context(tc.tile_pool(name="grpp", bufs=3))
+        w3q = ctx.enter_context(tc.tile_pool(name="w3q", bufs=3))
+        xp = ctx.enter_context(tc.tile_pool(name="xp", bufs=3))
+        xq = ctx.enter_context(tc.tile_pool(name="xq", bufs=2))
+        h3p = ctx.enter_context(tc.tile_pool(name="h3p", bufs=3))
+        h3q = ctx.enter_context(tc.tile_pool(name="h3q", bufs=2))
+        w4p = ctx.enter_context(tc.tile_pool(name="w4p", bufs=3))
+        w4q = ctx.enter_context(tc.tile_pool(name="w4q", bufs=2))
+        psx = ctx.enter_context(tc.psum_pool(name="psx", bufs=2))
+        ps1 = ctx.enter_context(tc.psum_pool(name="ps1", bufs=4))
+        ps2 = ctx.enter_context(tc.psum_pool(name="ps2", bufs=2))
+
+        warm = const.tile([P, 1], F32)
+        nc.vector.memset(warm[:], 0.0)
+        warm2 = const.tile([P, 1], F32)
+        nc.scalar.activation(out=warm2[:], in_=warm[:], func=ACT.Silu)
+
+        ident = const.tile([P, P], F32)
+        make_identity(nc, ident[:])
+
+        b3row = const.tile([P, P], BF16)
+        nc.vector.memset(b3row[:], 0.0)
+        nc.sync.dma_start(out=b3row[0:64, :], in_=b3v)
+        b4bc = const.tile([P, E * D], BF16)
+        nc.gpsimd.dma_start(out=b4bc[:], in_=b4.rearrange("e d -> (e d)").partition_broadcast(P))
+        b3f = const.tile([P, P], F32)
+        nc.vector.tensor_copy(out=b3f[:], in_=b3row[:])
+        b3ps = psx.tile([P, 512], F32, tag="xt")
+        nc.tensor.transpose(b3ps[:, 0:P], b3f[:], ident[:])
+        b3T = const.tile([P, 64], F32)
+        nc.vector.tensor_copy(out=b3T[:], in_=b3ps[:, 0:64])
+
+        out_sb = const.tile([P, 2 * E * D], F32)
+        out_v = out_sb[:].rearrange("p (bt e d) -> p bt e d", bt=2, e=E)
+
+        for e in range(E):
+            x_sb = xp.tile([P, 2 * H], BF16)
+            nc.sync.dma_start(out=x_sb[:].rearrange("p (bt k) -> p bt k", bt=2), in_=h2v[e])
+            raws = []
+            for g in range(2):
+                raw = rawp.tile([P, 4 * H], BF16)
+                nc.sync.dma_start(out=raw[:].rearrange("p (u x) -> p u x", u=2), in_=w3v[e, g])
+                raws.append(raw)
+            w4raw = w4p.tile([P, 8 * D], BF16)
+            nc.sync.dma_start(out=w4raw[:].rearrange("p (a d) -> p a d", a=8), in_=w4v[e])
+
+            x32 = x_sb[:].bitcast(F32)
+            xg = xq.tile([P, 2048], BF16, align_bytes=64)
+            xg32 = xg[:].bitcast(F32)
+            for g in range(2):
+                xt = psx.tile([P, 512], F32, tag="xt")
+                for u in range(2):
+                    for bt in range(2):
+                        nc.tensor.transpose(
+                            xt[:, u * 256 + bt * P : u * 256 + bt * P + P],
+                            x32[:, bt * 512 + 256 * g + P * u : bt * 512 + 256 * g + P * u + P],
+                            ident[:],
+                        )
+                dst = xg32[:, 512 * g : 512 * g + 512].rearrange("p (b u) -> p b u", u=2)
+                src = xt[:].rearrange("p (u b) -> p b u", u=2)
+                if g == 0:
+                    nc.scalar.copy(out=dst, in_=src)
+                else:
+                    nc.vector.tensor_copy(out=dst, in_=src)
+            xc = xq.tile([P, 512], U32, align_bytes=64)
+            xs = xq.tile([P, 512], U8, align_bytes=64)
+            nc.vector.quantize_mx(out=xc[:].bitcast(FP8X4), scales=xs[:], in_=xg[:])
+
+            w4g = w4q.tile([P, 1024], BF16, align_bytes=64)
+            for g in range(2):
+                dst, src = regroup_views(
+                    w4g[:, 512 * g : 512 * g + 512],
+                    w4raw[:, 512 * g : 512 * g + 512].rearrange("p (t d) -> p t d", t=4),
+                )
+                nc.vector.tensor_copy(out=dst, in_=src)
+            w4c = w4q.tile([P, 256], U32, align_bytes=64)
+            w4s = w4q.tile([P, 256], U8, align_bytes=64)
+            nc.vector.quantize_mx(out=w4c[:].bitcast(FP8X4), scales=w4s[:], in_=w4g[:])
+
+            h3c = h3q.tile([P, 512], U32, align_bytes=64)
+            h3s = h3q.tile([P, 512], U8, align_bytes=64)
+            for h in range(2):
+                grp = grpp.tile([P, 4096], BF16, align_bytes=64)
+                for g in range(2):
+                    dst, src = regroup_views(
+                        grp[:, 2048 * g : 2048 * g + 2048],
+                        raws[g][:].rearrange("p (t n) -> p t n", t=4)[:, :, 512 * h : 512 * h + 512],
+                    )
+                    if g == 0:
+                        nc.vector.tensor_copy(out=dst, in_=src)
+                    else:
+                        nc.scalar.copy(out=dst, in_=src)
+                w3c = w3q.tile([P, 1024], U32, align_bytes=64)
+                w3s = w3q.tile([P, 1024], U8, align_bytes=64)
+                nc.vector.quantize_mx(out=w3c[:].bitcast(FP8X4), scales=w3s[:], in_=grp[:])
+
+                a3 = h3p.tile([P, 1024], BF16)
+                for pair in range(2):
+                    acc = ps1.tile([P, 512], F32)
+                    for i in range(2):
+                        j = 2 * pair + i
+                        for g in range(2):
+                            cols = slice(512 * g + P * j, 512 * g + P * j + P)
+                            nc.tensor.matmul_mx(
+                                out=acc[:, 256 * i : 256 * i + 256],
+                                lhsT=w3c[:, cols].bitcast(FP8X4),
+                                lhsT_scale=w3s[:, cols],
+                                rhs=xc[:, 256 * g : 256 * g + 256].bitcast(FP8X4),
+                                rhs_scale=xs[:, 256 * g : 256 * g + 256],
+                                start=(g == 0),
+                                stop=(g == 1),
+                            )
+                    for i in range(2):
+                        j = 2 * pair + i
+                        col = e * 8 + 4 * h + j
+                        nc.scalar.activation(
+                            out=a3[:, 256 * j : 256 * j + 256],
+                            in_=acc[:, 256 * i : 256 * i + 256],
+                            func=ACT.Silu,
+                            bias=b3T[:, col : col + 1],
+                            scale=1.0,
+                        )
+                g3 = h3p.tile([P, 1024], BF16, align_bytes=64)
+                dst, src = regroup_views(g3[:], a3[:].rearrange("p (t b) -> p t b", t=4))
+                nc.vector.tensor_copy(out=dst, in_=src)
+                nc.vector.quantize_mx(
+                    out=h3c[:, 256 * h : 256 * h + 256].bitcast(FP8X4),
+                    scales=h3s[:, 256 * h : 256 * h + 256],
+                    in_=g3[:],
+                )
+
+            acc2 = ps2.tile([P, 256], F32)
+            for bt in range(2):
+                for g in range(2):
+                    cols = slice(256 * g + P * bt, 256 * g + P * bt + P)
+                    nc.tensor.matmul_mx(
+                        out=acc2[:, P * bt : P * bt + P],
+                        lhsT=h3c[:, cols].bitcast(FP8X4),
+                        lhsT_scale=h3s[:, cols],
+                        rhs=w4c[:, P * g : P * g + P].bitcast(FP8X4),
+                        rhs_scale=w4s[:, P * g : P * g + P],
+                        start=(g == 0),
+                        stop=(g == 1),
+                    )
+            nc.vector.tensor_tensor(
+                out=out_v[:, :, e, :],
+                in0=acc2[:].rearrange("p (bt d) -> p bt d", bt=2),
+                in1=b4bc[:, D * e : D * e + D].unsqueeze(1).to_broadcast([P, 2, D]),
+                op=ALU.add,
+            )
+            nc.sync.dma_start(out=outv[e], in_=out_v[:, :, e, :])

@@ -14,6 +14,7 @@ ALU = mybir.AluOpType
 P = 128
 B, E, D, H = 256, 8, 128, 1024
 FLOPS = 2 * E * B * H * (H + D)
+NS = 2 * E
 
 
 def regroup_views(dst, src):
@@ -25,147 +26,189 @@ def regroup_views(dst, src):
 
 def tile_environvectorfield_pb_kernel(tc, h2, W3, b3, W4, b4, out):
     nc = tc.nc
-    h2v = h2.rearrange("(p bt) e k -> e p bt k", bt=2)
-    w3v = W3.rearrange("e (g u p r) n -> e g p u (r n)", g=2, u=2, p=P, r=2)
+    h2one = h2.rearrange("(p bt) e k -> e p bt k", bt=2)
+    h2two = h2.rearrange("(p bt) (q f) k -> q p bt (f k)", bt=2, f=2)
+    w3whole = W3.rearrange("e (g p j) n -> e g p (j n)", g=2, p=P, j=4)
+    w3rows = W3.rearrange("e (g p j) n -> e g p j n", g=2, p=P, j=4)
     w4v = W4.rearrange("e (a p) d -> e p a d", p=P)
     b3v = b3.rearrange("e (j q) -> (e j) q", q=P)
-    outv = out.rearrange("(p bt e) d -> e p bt d", bt=2, e=E)
+    b4v = b4.rearrange("(o e) d -> o (e d)", o=1)
+    outv = out.rearrange("(p bt e) d -> p bt (e d)", bt=2, e=E)
 
     with ExitStack() as ctx:
         const = ctx.enter_context(tc.tile_pool(name="const", bufs=1))
         rawp = ctx.enter_context(tc.tile_pool(name="rawp", bufs=8))
         grpp = ctx.enter_context(tc.tile_pool(name="grpp", bufs=3))
         w3q = ctx.enter_context(tc.tile_pool(name="w3q", bufs=3))
-        xp = ctx.enter_context(tc.tile_pool(name="xp", bufs=3))
+        xp = ctx.enter_context(tc.tile_pool(name="xp", bufs=4))
         xq = ctx.enter_context(tc.tile_pool(name="xq", bufs=2))
         h3p = ctx.enter_context(tc.tile_pool(name="h3p", bufs=3))
         h3q = ctx.enter_context(tc.tile_pool(name="h3q", bufs=2))
-        w4p = ctx.enter_context(tc.tile_pool(name="w4p", bufs=3))
-        w4q = ctx.enter_context(tc.tile_pool(name="w4q", bufs=2))
+        w4p = ctx.enter_context(tc.tile_pool(name="w4p", bufs=8))
+        w4q = ctx.enter_context(tc.tile_pool(name="w4q", bufs=3))
         psx = ctx.enter_context(tc.psum_pool(name="psx", bufs=2))
         ps1 = ctx.enter_context(tc.psum_pool(name="ps1", bufs=4))
         ps2 = ctx.enter_context(tc.psum_pool(name="ps2", bufs=2))
+        ctx.enter_context(tc.manual_schedule())
 
-        warm = const.tile([P, 1], F32)
-        nc.vector.memset(warm[:], 0.0)
-        warm2 = const.tile([P, 1], F32)
-        nc.scalar.activation(out=warm2[:], in_=warm[:], func=ACT.Silu)
+        st = {}
 
-        ident = const.tile([P, P], F32)
-        make_identity(nc, ident[:])
+        def load_w3_piece(g, h):
+            raw = rawp.tile([P, 2048], BF16, name="raw", tag="raw")
+            nc.sync.dma_start(
+                out=raw[:].rearrange("p (j n) -> p j n", j=4),
+                in_=w3rows[0, g][:, :, 512 * h : 512 * h + 512],
+            )
+            st[("raw", 0, g, h)] = raw[:].rearrange("p (j n) -> p j n", j=4)
 
-        b3row = const.tile([P, P], BF16)
-        nc.vector.memset(b3row[:], 0.0)
-        nc.sync.dma_start(out=b3row[0:64, :], in_=b3v)
-        b4bc = const.tile([P, E * D], BF16)
-        nc.gpsimd.dma_start(out=b4bc[:], in_=b4.rearrange("e d -> (e d)").partition_broadcast(P))
-        b3f = const.tile([P, P], F32)
-        nc.vector.tensor_copy(out=b3f[:], in_=b3row[:])
-        b3ps = psx.tile([P, 512], F32, tag="xt")
-        nc.tensor.transpose(b3ps[:, 0:P], b3f[:], ident[:])
-        b3T = const.tile([P, 64], F32)
-        nc.vector.tensor_copy(out=b3T[:], in_=b3ps[:, 0:64])
+        def load_w3(e, g):
+            raw = rawp.tile([P, 4096], BF16, name="raw", tag="raw")
+            nc.sync.dma_start(out=raw[:], in_=w3whole[e, g])
+            rows = raw[:].rearrange("p (j n) -> p j n", j=4)
+            for h in range(2):
+                st[("raw", e, g, h)] = rows[:, :, 512 * h : 512 * h + 512]
 
-        out_sb = const.tile([P, 2 * E * D], F32)
-        out_v = out_sb[:].rearrange("p (bt e d) -> p bt e d", bt=2, e=E)
+        def x_tile(q):
+            x_sb = xp.tile([P, 4096], BF16, name="x_sb", tag="x_sb")
+            st[("x", q)] = x_sb
+            return x_sb
 
-        for e in range(E):
-            x_sb = xp.tile([P, 2 * H], BF16)
-            nc.sync.dma_start(out=x_sb[:].rearrange("p (bt k) -> p bt k", bt=2), in_=h2v[e])
-            raws = []
-            for g in range(2):
-                raw = rawp.tile([P, 4 * H], BF16)
-                nc.sync.dma_start(out=raw[:].rearrange("p (u x) -> p u x", u=2), in_=w3v[e, g])
-                raws.append(raw)
-            w4raw = w4p.tile([P, 8 * D], BF16)
+        def load_x_one(e):
+            x_sb = st[("x", e // 2)]
+            nc.sync.dma_start(
+                out=x_sb[:].rearrange("p (bt f k) -> p bt f k", bt=2, f=2)[:, :, e % 2, :],
+                in_=h2one[e],
+            )
+
+        def load_x_two(q):
+            x_sb = x_tile(q)
+            nc.sync.dma_start(out=x_sb[:].rearrange("p (bt x) -> p bt x", bt=2), in_=h2two[q])
+
+        def load_w4(e):
+            w4raw = w4p.tile([P, 8 * D], BF16, name="w4raw", tag="w4raw")
             nc.sync.dma_start(out=w4raw[:].rearrange("p (a d) -> p a d", a=8), in_=w4v[e])
+            st[("w4raw", e)] = w4raw
 
-            x32 = x_sb[:].bitcast(F32)
-            xg = xq.tile([P, 2048], BF16, align_bytes=64)
-            xg32 = xg[:].bitcast(F32)
+        def x_transposes(e):
+            x32 = st[("x", e // 2)][:].bitcast(F32)
             for g in range(2):
-                xt = psx.tile([P, 512], F32, tag="xt")
+                xt = psx.tile([P, 512], F32, name="xt", tag="xt")
                 for u in range(2):
                     for bt in range(2):
+                        base = bt * 1024 + (e % 2) * 512 + 256 * g
                         nc.tensor.transpose(
                             xt[:, u * 256 + bt * P : u * 256 + bt * P + P],
-                            x32[:, bt * 512 + 256 * g + P * u : bt * 512 + 256 * g + P * u + P],
+                            x32[:, base : base + 256].rearrange("p (w u) -> p u w", u=2)[:, u, :],
                             ident[:],
                         )
-                dst = xg32[:, 512 * g : 512 * g + 512].rearrange("p (b u) -> p b u", u=2)
-                src = xt[:].rearrange("p (u b) -> p b u", u=2)
-                if g == 0:
-                    nc.scalar.copy(out=dst, in_=src)
-                else:
-                    nc.vector.tensor_copy(out=dst, in_=src)
-            xc = xq.tile([P, 512], U32, align_bytes=64)
-            xs = xq.tile([P, 512], U8, align_bytes=64)
-            nc.vector.quantize_mx(out=xc[:].bitcast(FP8X4), scales=xs[:], in_=xg[:])
+                st[("xt", e, g)] = xt
 
-            w4g = w4q.tile([P, 1024], BF16, align_bytes=64)
+        def x_copies(e):
+            xg = xq.tile([P, 2048], BF16, name="xg", tag="xg", align_bytes=64)
+            xg32 = xg[:].bitcast(F32)
+            for g in range(2):
+                nc.scalar.copy(
+                    out=xg32[:, 512 * g : 512 * g + 512].rearrange("p (b u) -> p b u", u=2),
+                    in_=st[("xt", e, g)][:].rearrange("p (u b) -> p b u", u=2),
+                )
+            st[("xg", e)] = xg
+
+        def x_quantise(e):
+            xc = xq.tile([P, 512], U32, name="xc", tag="xc", align_bytes=64)
+            xs = xq.tile([P, 512], U8, name="xs", tag="xs", align_bytes=64)
+            nc.vector.quantize_mx(out=xc[:].bitcast(FP8X4), scales=xs[:], in_=st[("xg", e)][:])
+            st[("xc", e)] = (xc, xs)
+
+        def w3_regroup(s, g, engine):
+            if ("grp", s) not in st:
+                grp_new = grpp.tile([P, 4096], BF16, name="grp", tag="grp", align_bytes=64)
+                st[("grp", s)] = grp_new
+            grp = st[("grp", s)]
+            dst, src = regroup_views(grp[:, 2048 * g : 2048 * g + 2048], st[("raw", s // 2, g, s % 2)])
+            if engine == "V":
+                nc.vector.tensor_copy(out=dst, in_=src)
+            else:
+                nc.scalar.copy(out=dst, in_=src)
+
+        def w3_quantise(s):
+            w3c = w3q.tile([P, 1024], U32, name="w3c", tag="w3c", align_bytes=64)
+            w3s = w3q.tile([P, 1024], U8, name="w3s", tag="w3s", align_bytes=64)
+            nc.vector.quantize_mx(out=w3c[:].bitcast(FP8X4), scales=w3s[:], in_=st[("grp", s)][:])
+            st[("w3c", s)] = (w3c, w3s)
+
+        def stage1(s):
+            w3c, w3s = st[("w3c", s)]
+            xc, xs = st[("xc", s // 2)]
+            for pair in range(2):
+                acc = ps1.tile([P, 512], F32, name="acc", tag="acc")
+                for i in range(2):
+                    j = 2 * pair + i
+                    for g in range(2):
+                        cols = slice(512 * g + P * j, 512 * g + P * j + P)
+                        nc.tensor.matmul_mx(
+                            out=acc[:, 256 * i : 256 * i + 256],
+                            lhsT=w3c[:, cols].bitcast(FP8X4),
+                            lhsT_scale=w3s[:, cols],
+                            rhs=xc[:, 256 * g : 256 * g + 256].bitcast(FP8X4),
+                            rhs_scale=xs[:, 256 * g : 256 * g + 256],
+                            start=(g == 0),
+                            stop=(g == 1),
+                        )
+                st[("acc", s, pair)] = acc
+
+        def swish(s):
+            a3 = h3p.tile([P, 1024], BF16, name="a3", tag="a3")
+            for j in range(4):
+                col = 4 * s + j
+                nc.scalar.activation(
+                    out=a3[:, 256 * j : 256 * j + 256],
+                    in_=st[("acc", s, j // 2)][:, 256 * (j % 2) : 256 * (j % 2) + 256],
+                    func=ACT.Silu,
+                    bias=b3T[:, col : col + 1],
+                    scale=1.0,
+                )
+            st[("a3", s)] = a3
+
+        def h3_regroup(s):
+            g3 = h3p.tile([P, 1024], BF16, name="g3", tag="g3", align_bytes=64)
+            dst, src = regroup_views(g3[:], st[("a3", s)][:].rearrange("p (t b) -> p t b", t=4))
+            nc.vector.tensor_copy(out=dst, in_=src)
+            st[("g3", s)] = g3
+
+        def h3_quantise(s):
+            if s % 2 == 0:
+                h3c_new = h3q.tile([P, 512], U32, name="h3c", tag="h3c", align_bytes=64)
+                h3s_new = h3q.tile([P, 512], U8, name="h3s", tag="h3s", align_bytes=64)
+                st[("h3c", s // 2)] = (h3c_new, h3s_new)
+            h3c, h3s = st[("h3c", s // 2)]
+            h = s % 2
+            nc.vector.quantize_mx(
+                out=h3c[:, 256 * h : 256 * h + 256].bitcast(FP8X4),
+                scales=h3s[:, 256 * h : 256 * h + 256],
+                in_=st[("g3", s)][:],
+            )
+
+        def w4_regroup(e):
+            w4raw = st[("w4raw", e)]
+            w4g = w4q.tile([P, 1024], BF16, name="w4g", tag="w4g", align_bytes=64)
             for g in range(2):
                 dst, src = regroup_views(
                     w4g[:, 512 * g : 512 * g + 512],
                     w4raw[:, 512 * g : 512 * g + 512].rearrange("p (t d) -> p t d", t=4),
                 )
                 nc.vector.tensor_copy(out=dst, in_=src)
-            w4c = w4q.tile([P, 256], U32, align_bytes=64)
-            w4s = w4q.tile([P, 256], U8, align_bytes=64)
-            nc.vector.quantize_mx(out=w4c[:].bitcast(FP8X4), scales=w4s[:], in_=w4g[:])
+            st[("w4g", e)] = w4g
 
-            h3c = h3q.tile([P, 512], U32, align_bytes=64)
-            h3s = h3q.tile([P, 512], U8, align_bytes=64)
-            for h in range(2):
-                grp = grpp.tile([P, 4096], BF16, align_bytes=64)
-                for g in range(2):
-                    dst, src = regroup_views(
-                        grp[:, 2048 * g : 2048 * g + 2048],
-                        raws[g][:].rearrange("p (t n) -> p t n", t=4)[:, :, 512 * h : 512 * h + 512],
-                    )
-                    if g == 0:
-                        nc.vector.tensor_copy(out=dst, in_=src)
-                    else:
-                        nc.scalar.copy(out=dst, in_=src)
-                w3c = w3q.tile([P, 1024], U32, align_bytes=64)
-                w3s = w3q.tile([P, 1024], U8, align_bytes=64)
-                nc.vector.quantize_mx(out=w3c[:].bitcast(FP8X4), scales=w3s[:], in_=grp[:])
+        def w4_quantise(e):
+            w4c = w4q.tile([P, 256], U32, name="w4c", tag="w4c", align_bytes=64)
+            w4s = w4q.tile([P, 256], U8, name="w4s", tag="w4s", align_bytes=64)
+            nc.vector.quantize_mx(out=w4c[:].bitcast(FP8X4), scales=w4s[:], in_=st[("w4g", e)][:])
+            st[("w4c", e)] = (w4c, w4s)
 
-                a3 = h3p.tile([P, 1024], BF16)
-                for pair in range(2):
-                    acc = ps1.tile([P, 512], F32)
-                    for i in range(2):
-                        j = 2 * pair + i
-                        for g in range(2):
-                            cols = slice(512 * g + P * j, 512 * g + P * j + P)
-                            nc.tensor.matmul_mx(
-                                out=acc[:, 256 * i : 256 * i + 256],
-                                lhsT=w3c[:, cols].bitcast(FP8X4),
-                                lhsT_scale=w3s[:, cols],
-                                rhs=xc[:, 256 * g : 256 * g + 256].bitcast(FP8X4),
-                                rhs_scale=xs[:, 256 * g : 256 * g + 256],
-                                start=(g == 0),
-                                stop=(g == 1),
-                            )
-                    for i in range(2):
-                        j = 2 * pair + i
-                        col = e * 8 + 4 * h + j
-                        nc.scalar.activation(
-                            out=a3[:, 256 * j : 256 * j + 256],
-                            in_=acc[:, 256 * i : 256 * i + 256],
-                            func=ACT.Silu,
-                            bias=b3T[:, col : col + 1],
-                            scale=1.0,
-                        )
-                g3 = h3p.tile([P, 1024], BF16, align_bytes=64)
-                dst, src = regroup_views(g3[:], a3[:].rearrange("p (t b) -> p t b", t=4))
-                nc.vector.tensor_copy(out=dst, in_=src)
-                nc.vector.quantize_mx(
-                    out=h3c[:, 256 * h : 256 * h + 256].bitcast(FP8X4),
-                    scales=h3s[:, 256 * h : 256 * h + 256],
-                    in_=g3[:],
-                )
-
-            acc2 = ps2.tile([P, 256], F32)
+        def stage2(e):
+            h3c, h3s = st[("h3c", e)]
+            w4c, w4s = st[("w4c", e)]
+            acc2 = ps2.tile([P, 256], F32, name="acc2", tag="acc2")
             for bt in range(2):
                 for g in range(2):
                     cols = slice(256 * g + P * bt, 256 * g + P * bt + P)
@@ -178,10 +221,138 @@ def tile_environvectorfield_pb_kernel(tc, h2, W3, b3, W4, b4, out):
                         start=(g == 0),
                         stop=(g == 1),
                     )
+            st[("acc2", e)] = acc2
+
+        def add_bias(e):
             nc.vector.tensor_tensor(
                 out=out_v[:, :, e, :],
-                in0=acc2[:].rearrange("p (bt d) -> p bt d", bt=2),
+                in0=st[("acc2", e)][:].rearrange("p (bt d) -> p bt d", bt=2),
                 in1=b4bc[:, D * e : D * e + D].unsqueeze(1).to_broadcast([P, 2, D]),
                 op=ALU.add,
             )
-            nc.sync.dma_start(out=outv[e], in_=out_v[:, :, e, :])
+
+        def store(e0, e1):
+            nc.sync.dma_start(
+                out=outv[:, :, D * e0 : D * e1],
+                in_=out_sb[:].rearrange("p (bt x) -> p bt x", bt=2)[:, :, D * e0 : D * e1],
+            )
+
+        b3row = const.tile([P, P], BF16)
+        nc.vector.memset(b3row[:], 0.0)
+        b4z = const.tile([P, E * D], BF16)
+        nc.vector.memset(b4z[:], 0.0)
+        ones = const.tile([P, P], BF16)
+        nc.vector.memset(ones[:], 1.0)
+        warm = const.tile([P, 1], F32)
+        nc.vector.memset(warm[:], 0.0)
+        nc.scalar.dma_start(out=b4z[0:1, :], in_=b4v)
+        nc.scalar.dma_start(out=b3row[0:64, :], in_=b3v)
+        warm2 = const.tile([P, 1], F32)
+        nc.scalar.activation(out=warm2[:], in_=warm[:], func=ACT.Silu)
+        ident = const.tile([P, P], F32)
+        make_identity(nc, ident[:])
+
+        load_w3_piece(0, 0)
+        load_w3_piece(1, 0)
+        x_tile(0)
+        load_x_one(0)
+        load_w3_piece(0, 1)
+        load_w3_piece(1, 1)
+        load_w3(1, 0)
+        load_x_one(1)
+        load_w3(1, 1)
+        load_x_two(1)
+        load_w4(0)
+        load_w3(2, 0)
+        load_w3(2, 1)
+        load_w4(1)
+
+        b4bc = const.tile([P, E * D], F32)
+        b3f = const.tile([P, P], F32)
+        b3T = const.tile([P, 64], F32)
+
+        def b3_transpose():
+            nc.vector.tensor_copy(out=b3f[:], in_=b3row[:])
+            b3ps = ps2.tile([P, 256], F32, name="b3ps", tag="acc2")
+            nc.tensor.transpose(b3ps[:, 0:P], b3f[:], ident[:])
+            st["b3ps"] = b3ps
+
+        def b3_copy():
+            nc.vector.tensor_copy(out=b3T[:], in_=st["b3ps"][:, 0:64])
+
+        def b4_spread():
+            for c in range(4):
+                b4ps = ps2.tile([P, 256], F32, name="b4ps", tag="acc2")
+                nc.tensor.matmul(b4ps[:], lhsT=ones[:], rhs=b4z[:, 256 * c : 256 * c + 256], start=True, stop=True)
+                if c % 2 == 0:
+                    nc.vector.tensor_copy(out=b4bc[:, 256 * c : 256 * c + 256], in_=b4ps[:])
+                else:
+                    nc.scalar.copy(out=b4bc[:, 256 * c : 256 * c + 256], in_=b4ps[:])
+
+        out_sb = const.tile([P, 2 * E * D], F32)
+        out_v = out_sb[:].rearrange("p (bt e d) -> p bt e d", bt=2, e=E)
+
+        later_loads = {
+            1: [("w3", 3), ("w4", 2), ("x", 2)],
+            2: [("w3", 4), ("w4", 3)],
+            4: [("w3", 5), ("w4", 4), ("x", 3)],
+            6: [("w3", 6), ("w4", 5)],
+            8: [("w3", 7), ("w4", 6), ("w4", 7)],
+        }
+        x_t_step = {0: 0, 1: 1}
+        x_q_step = {0: 1, 1: 2}
+        for e in range(2, E):
+            x_t_step[e] = 2 * e - 2
+            x_q_step[e] = 2 * e - 1
+        stores_after = {3: (0, 4), 5: (4, 6), 6: (6, 7), 7: (7, 8)}
+
+        for s in range(NS + 6):
+            for kind, idx in later_loads.get(s, []):
+                if kind == "w3":
+                    load_w3(idx, 0)
+                    load_w3(idx, 1)
+                elif kind == "w4":
+                    load_w4(idx)
+                else:
+                    load_x_two(idx)
+            for e in range(E):
+                if x_t_step[e] == s:
+                    x_transposes(e)
+            if s == 2:
+                b3_transpose()
+            if 0 <= s - 1 < NS:
+                w3_quantise(s - 1)
+            if s < NS:
+                w3_regroup(s, 1, "S")
+            if 0 <= s - 3 < NS:
+                h3_regroup(s - 3)
+            if s < NS:
+                w3_regroup(s, 0, "V")
+            if s == 2:
+                b3_copy()
+            for e in range(E):
+                if x_q_step[e] == s:
+                    x_quantise(e)
+            if 0 <= s - 1 < NS:
+                stage1(s - 1)
+            if 0 <= s - 2 < NS:
+                swish(s - 2)
+            for e in range(E):
+                if x_t_step[e] == s:
+                    x_copies(e)
+            if 0 <= s - 3 < NS:
+                h3_quantise(s - 3)
+                if (s - 3) % 2 == 1:
+                    stage2((s - 3) // 2)
+            if s == 3:
+                b4_spread()
+            if s % 2 == 0 and 0 <= s // 2 - 1 < E:
+                w4_regroup(s // 2 - 1)
+            if s % 2 == 1:
+                if 0 <= s // 2 - 1 < E:
+                    w4_quantise(s // 2 - 1)
+                ea = (s - 5) // 2
+                if 0 <= ea < E:
+                    add_bias(ea)
+                    if ea in stores_after:
+                        store(stores_after[ea][0], stores_after[ea][1])

@@ -14,7 +14,52 @@ ALU = mybir.AluOpType
 P = 128
 B, E, D, H = 256, 8, 128, 1024
 FLOPS = 2 * E * B * H * (H + D)
-NS = 2 * E
+
+PROGRAM = (
+    ("LWP", 0, 0), ("LWP", 1, 0), ("LB3",), ("LB4",), ("LX1", 0), ("R", 0, 0, "V"),
+    ("LWP", 0, 1), ("R", 0, 1, "V"), ("LWP", 1, 1), ("B3A",), ("Q", 0), ("XT", 0),
+    ("LW", 1, 0), ("B3T",), ("R", 1, 0, "V"), ("XC", 0, 0, "S"), ("XC", 0, 1, "S"), ("B3C",),
+    ("LX1", 1), ("R", 1, 1, "V"), ("B4M", 0), ("B4M", 1), ("B4C", 1, "S"), ("XQ", 0),
+    ("LW", 1, 1), ("B4M", 3), ("B4C", 0, "V"), ("B4C", 3, "S"), ("Q", 1), ("R", 2, 0, "S"),
+    ("M", 0, 0), ("B4M", 2), ("R", 3, 0, "V"), ("M", 0, 1), ("LX2", 1), ("XT", 1),
+    ("B4C", 2, "V"), ("A", 0, 0), ("A", 0, 1), ("M", 1, 0), ("XC", 1, 0, "S"), ("R", 2, 1, "V"),
+    ("LW4", 0), ("M", 1, 1), ("XC", 1, 1, "S"), ("R", 3, 1, "S"), ("Q", 2), ("LW", 2, 0),
+    ("XQ", 1), ("XT", 2), ("H", 0), ("A", 1, 0), ("LW", 2, 1), ("W4R", 0),
+    ("M", 2, 0), ("XC", 2, 0, "S"), ("Q", 3), ("M", 2, 1), ("XC", 2, 1, "S"), ("A", 1, 1),
+    ("XT", 3), ("XQ", 2), ("A", 2, 0), ("LW4", 1), ("H", 1), ("R", 4, 0, "S"),
+    ("M", 3, 0), ("HQ", 0), ("W4Q", 0), ("LW", 3, 0), ("HQ", 1), ("M", 3, 1),
+    ("R", 5, 0, "V"), ("O", 0), ("R", 4, 1, "S"), ("R", 5, 1, "V"), ("LW", 3, 1), ("ADD", 0),
+    ("W4R", 1), ("A", 2, 1), ("Q", 5), ("XC", 3, 0, "S"), ("LW4", 2), ("R", 6, 0, "S"),
+    ("Q", 4), ("LX2", 2), ("H", 2), ("M", 4, 0), ("HQ", 2), ("R", 6, 1, "S"),
+    ("W4Q", 1), ("R", 7, 0, "V"), ("M", 4, 1), ("LW", 4, 0), ("W4R", 2), ("R", 7, 1, "V"),
+    ("XC", 3, 1, "S"), ("A", 3, 0), ("LW", 4, 1), ("XT", 4), ("XQ", 3), ("A", 3, 1),
+    ("Q", 6), ("A", 4, 0), ("M", 5, 0), ("A", 4, 1), ("H", 3), ("M", 5, 1),
+    ("XC", 4, 0, "S"), ("LW4", 3), ("H", 4), ("R", 8, 0, "S"), ("M", 6, 0), ("Q", 7),
+    ("LW", 5, 0), ("M", 6, 1), ("HQ", 3), ("HQ", 4), ("R", 8, 1, "S"), ("W4Q", 2),
+    ("O", 1), ("R", 9, 0, "V"), ("LW", 5, 1), ("ADD", 1), ("W4R", 3), ("XC", 4, 1, "S"),
+    ("Q", 8), ("A", 5, 0), ("XT", 5), ("LW4", 4), ("A", 5, 1), ("XQ", 4),
+    ("R", 9, 1, "S"), ("LX2", 3), ("M", 7, 0), ("H", 5), ("HQ", 5), ("M", 7, 1),
+    ("W4Q", 3), ("R", 10, 0, "V"), ("O", 2), ("A", 6, 0), ("LW", 6, 0), ("Q", 9),
+    ("A", 6, 1), ("M", 8, 0), ("R", 10, 1, "S"), ("ADD", 2), ("M", 8, 1), ("H", 6),
+    ("LW", 6, 1), ("W4R", 4), ("HQ", 6), ("XC", 5, 0, "S"), ("R", 11, 0, "V"), ("XC", 5, 1, "S"),
+    ("A", 7, 0), ("Q", 10), ("XT", 6), ("LW4", 5), ("A", 7, 1), ("R", 11, 1, "S"),
+    ("XQ", 5), ("M", 9, 0), ("LW", 7, 0), ("H", 7), ("M", 9, 1), ("HQ", 7),
+    ("W4Q", 4), ("R", 12, 0, "V"), ("O", 3), ("A", 8, 0), ("LW", 7, 1), ("A", 8, 1),
+    ("M", 10, 0), ("ADD", 3), ("R", 12, 1, "S"), ("Q", 11), ("M", 10, 1), ("H", 8),
+    ("LW4", 6), ("W4R", 5), ("XC", 6, 0, "S"), ("LW4", 7), ("Q", 12), ("XC", 6, 1, "S"),
+    ("A", 9, 0), ("ST", 0, 4), ("XT", 7), ("XQ", 6), ("A", 9, 1), ("HQ", 8),
+    ("R", 13, 0, "V"), ("R", 13, 1, "S"), ("M", 11, 0), ("M", 11, 1), ("H", 9), ("W4R", 6),
+    ("A", 10, 0), ("HQ", 9), ("Q", 13), ("A", 10, 1), ("M", 12, 0), ("R", 14, 0, "S"),
+    ("H", 10), ("O", 4), ("HQ", 10), ("M", 12, 1), ("ADD", 4), ("W4Q", 5),
+    ("R", 14, 1, "V"), ("XC", 7, 0, "S"), ("XC", 7, 1, "S"), ("Q", 14), ("A", 11, 0), ("A", 11, 1),
+    ("M", 13, 0), ("XQ", 7), ("R", 15, 0, "S"), ("H", 11), ("M", 13, 1), ("W4R", 7),
+    ("HQ", 11), ("R", 15, 1, "V"), ("A", 12, 0), ("O", 5), ("A", 12, 1), ("M", 14, 0),
+    ("Q", 15), ("A", 13, 0), ("M", 14, 1), ("A", 13, 1), ("ADD", 5), ("H", 12),
+    ("A", 14, 0), ("M", 15, 0), ("ST", 4, 6), ("H", 13), ("A", 14, 1), ("M", 15, 1),
+    ("HQ", 12), ("A", 15, 0), ("W4Q", 6), ("H", 14), ("A", 15, 1), ("HQ", 13),
+    ("HQ", 14), ("H", 15), ("O", 6), ("W4Q", 7), ("HQ", 15), ("ADD", 6),
+    ("O", 7), ("ST", 6, 7), ("ADD", 7), ("ST", 7, 8),
+)
 
 
 def regroup_views(dst, src):
@@ -53,6 +98,12 @@ def tile_environvectorfield_pb_kernel(tc, h2, W3, b3, W4, b4, out):
 
         st = {}
 
+        def copy_on(engine, dst, src):
+            if engine == "V":
+                nc.vector.tensor_copy(out=dst, in_=src)
+            else:
+                nc.scalar.copy(out=dst, in_=src)
+
         def load_w3_piece(g, h):
             raw = rawp.tile([P, 2048], BF16, name="raw", tag="raw")
             nc.sync.dma_start(
@@ -68,12 +119,10 @@ def tile_environvectorfield_pb_kernel(tc, h2, W3, b3, W4, b4, out):
             for h in range(2):
                 st[("raw", e, g, h)] = rows[:, :, 512 * h : 512 * h + 512]
 
-        def x_tile(q):
-            x_sb = xp.tile([P, 4096], BF16, name="x_sb", tag="x_sb")
-            st[("x", q)] = x_sb
-            return x_sb
-
         def load_x_one(e):
+            if ("x", e // 2) not in st:
+                x_new = xp.tile([P, 4096], BF16, name="x_sb", tag="x_sb")
+                st[("x", e // 2)] = x_new
             x_sb = st[("x", e // 2)]
             nc.sync.dma_start(
                 out=x_sb[:].rearrange("p (bt f k) -> p bt f k", bt=2, f=2)[:, :, e % 2, :],
@@ -81,13 +130,20 @@ def tile_environvectorfield_pb_kernel(tc, h2, W3, b3, W4, b4, out):
             )
 
         def load_x_two(q):
-            x_sb = x_tile(q)
+            x_sb = xp.tile([P, 4096], BF16, name="x_sb", tag="x_sb")
+            st[("x", q)] = x_sb
             nc.sync.dma_start(out=x_sb[:].rearrange("p (bt x) -> p bt x", bt=2), in_=h2two[q])
 
         def load_w4(e):
             w4raw = w4p.tile([P, 8 * D], BF16, name="w4raw", tag="w4raw")
             nc.sync.dma_start(out=w4raw[:].rearrange("p (a d) -> p a d", a=8), in_=w4v[e])
             st[("w4raw", e)] = w4raw
+
+        def load_b3():
+            nc.sync.dma_start(out=b3row[0:64, :], in_=b3v)
+
+        def load_b4():
+            nc.sync.dma_start(out=b4z[0:1, :], in_=b4v)
 
         def x_transposes(e):
             x32 = st[("x", e // 2)][:].bitcast(F32)
@@ -103,15 +159,16 @@ def tile_environvectorfield_pb_kernel(tc, h2, W3, b3, W4, b4, out):
                         )
                 st[("xt", e, g)] = xt
 
-        def x_copies(e):
-            xg = xq.tile([P, 2048], BF16, name="xg", tag="xg", align_bytes=64)
-            xg32 = xg[:].bitcast(F32)
-            for g in range(2):
-                nc.scalar.copy(
-                    out=xg32[:, 512 * g : 512 * g + 512].rearrange("p (b u) -> p b u", u=2),
-                    in_=st[("xt", e, g)][:].rearrange("p (u b) -> p b u", u=2),
-                )
-            st[("xg", e)] = xg
+        def x_copy(e, g, engine):
+            if ("xg", e) not in st:
+                xg_new = xq.tile([P, 2048], BF16, name="xg", tag="xg", align_bytes=64)
+                st[("xg", e)] = xg_new
+            xg32 = st[("xg", e)][:].bitcast(F32)
+            copy_on(
+                engine,
+                xg32[:, 512 * g : 512 * g + 512].rearrange("p (b u) -> p b u", u=2),
+                st[("xt", e, g)][:].rearrange("p (u b) -> p b u", u=2),
+            )
 
         def x_quantise(e):
             xc = xq.tile([P, 512], U32, name="xc", tag="xc", align_bytes=64)
@@ -125,10 +182,7 @@ def tile_environvectorfield_pb_kernel(tc, h2, W3, b3, W4, b4, out):
                 st[("grp", s)] = grp_new
             grp = st[("grp", s)]
             dst, src = regroup_views(grp[:, 2048 * g : 2048 * g + 2048], st[("raw", s // 2, g, s % 2)])
-            if engine == "V":
-                nc.vector.tensor_copy(out=dst, in_=src)
-            else:
-                nc.scalar.copy(out=dst, in_=src)
+            copy_on(engine, dst, src)
 
         def w3_quantise(s):
             w3c = w3q.tile([P, 1024], U32, name="w3c", tag="w3c", align_bytes=64)
@@ -136,38 +190,40 @@ def tile_environvectorfield_pb_kernel(tc, h2, W3, b3, W4, b4, out):
             nc.vector.quantize_mx(out=w3c[:].bitcast(FP8X4), scales=w3s[:], in_=st[("grp", s)][:])
             st[("w3c", s)] = (w3c, w3s)
 
-        def stage1(s):
+        def stage1(s, pair):
             w3c, w3s = st[("w3c", s)]
             xc, xs = st[("xc", s // 2)]
-            for pair in range(2):
-                acc = ps1.tile([P, 512], F32, name="acc", tag="acc")
-                for i in range(2):
-                    j = 2 * pair + i
-                    for g in range(2):
-                        cols = slice(512 * g + P * j, 512 * g + P * j + P)
-                        nc.tensor.matmul_mx(
-                            out=acc[:, 256 * i : 256 * i + 256],
-                            lhsT=w3c[:, cols].bitcast(FP8X4),
-                            lhsT_scale=w3s[:, cols],
-                            rhs=xc[:, 256 * g : 256 * g + 256].bitcast(FP8X4),
-                            rhs_scale=xs[:, 256 * g : 256 * g + 256],
-                            start=(g == 0),
-                            stop=(g == 1),
-                        )
-                st[("acc", s, pair)] = acc
+            acc = ps1.tile([P, 512], F32, name="acc", tag="acc")
+            for i in range(2):
+                j = 2 * pair + i
+                for g in range(2):
+                    cols = slice(512 * g + P * j, 512 * g + P * j + P)
+                    nc.tensor.matmul_mx(
+                        out=acc[:, 256 * i : 256 * i + 256],
+                        lhsT=w3c[:, cols].bitcast(FP8X4),
+                        lhsT_scale=w3s[:, cols],
+                        rhs=xc[:, 256 * g : 256 * g + 256].bitcast(FP8X4),
+                        rhs_scale=xs[:, 256 * g : 256 * g + 256],
+                        start=(g == 0),
+                        stop=(g == 1),
+                    )
+            st[("acc", s, pair)] = acc
 
-        def swish(s):
-            a3 = h3p.tile([P, 1024], BF16, name="a3", tag="a3")
-            for j in range(4):
+        def swish(s, pair):
+            if ("a3", s) not in st:
+                a3_new = h3p.tile([P, 1024], BF16, name="a3", tag="a3")
+                st[("a3", s)] = a3_new
+            a3 = st[("a3", s)]
+            for i in range(2):
+                j = 2 * pair + i
                 col = 4 * s + j
                 nc.scalar.activation(
                     out=a3[:, 256 * j : 256 * j + 256],
-                    in_=st[("acc", s, j // 2)][:, 256 * (j % 2) : 256 * (j % 2) + 256],
+                    in_=st[("acc", s, pair)][:, 256 * i : 256 * i + 256],
                     func=ACT.Silu,
                     bias=b3T[:, col : col + 1],
                     scale=1.0,
                 )
-            st[("a3", s)] = a3
 
         def h3_regroup(s):
             g3 = h3p.tile([P, 1024], BF16, name="g3", tag="g3", align_bytes=64)
@@ -176,7 +232,7 @@ def tile_environvectorfield_pb_kernel(tc, h2, W3, b3, W4, b4, out):
             st[("g3", s)] = g3
 
         def h3_quantise(s):
-            if s % 2 == 0:
+            if ("h3c", s // 2) not in st:
                 h3c_new = h3q.tile([P, 512], U32, name="h3c", tag="h3c", align_bytes=64)
                 h3s_new = h3q.tile([P, 512], U8, name="h3s", tag="h3s", align_bytes=64)
                 st[("h3c", s // 2)] = (h3c_new, h3s_new)
@@ -237,42 +293,10 @@ def tile_environvectorfield_pb_kernel(tc, h2, W3, b3, W4, b4, out):
                 in_=out_sb[:].rearrange("p (bt x) -> p bt x", bt=2)[:, :, D * e0 : D * e1],
             )
 
-        b3row = const.tile([P, P], BF16)
-        nc.vector.memset(b3row[:], 0.0)
-        b4z = const.tile([P, E * D], BF16)
-        nc.vector.memset(b4z[:], 0.0)
-        ones = const.tile([P, P], BF16)
-        nc.vector.memset(ones[:], 1.0)
-        warm = const.tile([P, 1], F32)
-        nc.vector.memset(warm[:], 0.0)
-        nc.scalar.dma_start(out=b4z[0:1, :], in_=b4v)
-        nc.scalar.dma_start(out=b3row[0:64, :], in_=b3v)
-        warm2 = const.tile([P, 1], F32)
-        nc.scalar.activation(out=warm2[:], in_=warm[:], func=ACT.Silu)
-        ident = const.tile([P, P], F32)
-        make_identity(nc, ident[:])
-
-        load_w3_piece(0, 0)
-        load_w3_piece(1, 0)
-        x_tile(0)
-        load_x_one(0)
-        load_w3_piece(0, 1)
-        load_w3_piece(1, 1)
-        load_w3(1, 0)
-        load_x_one(1)
-        load_w3(1, 1)
-        load_x_two(1)
-        load_w4(0)
-        load_w3(2, 0)
-        load_w3(2, 1)
-        load_w4(1)
-
-        b4bc = const.tile([P, E * D], F32)
-        b3f = const.tile([P, P], F32)
-        b3T = const.tile([P, 64], F32)
+        def b3_cast():
+            nc.vector.tensor_copy(out=b3f[:], in_=b3row[:])
 
         def b3_transpose():
-            nc.vector.tensor_copy(out=b3f[:], in_=b3row[:])
             b3ps = ps2.tile([P, 256], F32, name="b3ps", tag="acc2")
             nc.tensor.transpose(b3ps[:, 0:P], b3f[:], ident[:])
             st["b3ps"] = b3ps
@@ -280,79 +304,38 @@ def tile_environvectorfield_pb_kernel(tc, h2, W3, b3, W4, b4, out):
         def b3_copy():
             nc.vector.tensor_copy(out=b3T[:], in_=st["b3ps"][:, 0:64])
 
-        def b4_spread():
-            for c in range(4):
-                b4ps = ps2.tile([P, 256], F32, name="b4ps", tag="acc2")
-                nc.tensor.matmul(b4ps[:], lhsT=ones[:], rhs=b4z[:, 256 * c : 256 * c + 256], start=True, stop=True)
-                if c % 2 == 0:
-                    nc.vector.tensor_copy(out=b4bc[:, 256 * c : 256 * c + 256], in_=b4ps[:])
-                else:
-                    nc.scalar.copy(out=b4bc[:, 256 * c : 256 * c + 256], in_=b4ps[:])
+        def b4_matmul(c):
+            b4ps = ps2.tile([P, 256], F32, name="b4ps", tag="acc2")
+            nc.tensor.matmul(b4ps[:], lhsT=ones[:], rhs=b4z[:, 256 * c : 256 * c + 256], start=True, stop=True)
+            st[("b4ps", c)] = b4ps
 
+        def b4_copy(c, engine):
+            copy_on(engine, b4bc[:, 256 * c : 256 * c + 256], st[("b4ps", c)][:])
+
+        b4z = const.tile([P, E * D], BF16)
+        nc.gpsimd.memset(b4z[:].bitcast(F32), 0.0)
+        b3row = const.tile([P, P], BF16)
+        nc.gpsimd.memset(b3row[:].bitcast(F32), 0.0)
+        ident = const.tile([P, P], F32)
+        make_identity(nc, ident[:])
+        ones = const.tile([P, P], BF16)
+        nc.vector.memset(ones[:], 1.0)
+        warm = const.tile([P, 1], F32)
+        nc.vector.memset(warm[:], 0.0)
+        warm2 = const.tile([P, 1], F32)
+        nc.scalar.activation(out=warm2[:], in_=warm[:], func=ACT.Silu)
+        b4bc = const.tile([P, E * D], F32)
+        b3f = const.tile([P, P], F32)
+        b3T = const.tile([P, 64], F32)
         out_sb = const.tile([P, 2 * E * D], F32)
         out_v = out_sb[:].rearrange("p (bt e d) -> p bt e d", bt=2, e=E)
 
-        later_loads = {
-            1: [("w3", 3), ("w4", 2), ("x", 2)],
-            2: [("w3", 4), ("w4", 3)],
-            4: [("w3", 5), ("w4", 4), ("x", 3)],
-            6: [("w3", 6), ("w4", 5)],
-            8: [("w3", 7), ("w4", 6), ("w4", 7)],
+        emit = {
+            "LWP": load_w3_piece, "LW": load_w3, "LX1": load_x_one, "LX2": load_x_two, "LW4": load_w4,
+            "LB3": load_b3, "LB4": load_b4, "XT": x_transposes, "XC": x_copy, "XQ": x_quantise,
+            "R": w3_regroup, "Q": w3_quantise, "M": stage1, "A": swish, "H": h3_regroup, "HQ": h3_quantise,
+            "W4R": w4_regroup, "W4Q": w4_quantise, "O": stage2, "ADD": add_bias, "ST": store,
+            "B3A": b3_cast, "B3T": b3_transpose, "B3C": b3_copy, "B4M": b4_matmul, "B4C": b4_copy,
         }
-        x_t_step = {0: 0, 1: 1}
-        x_q_step = {0: 1, 1: 2}
-        for e in range(2, E):
-            x_t_step[e] = 2 * e - 2
-            x_q_step[e] = 2 * e - 1
-        stores_after = {3: (0, 4), 5: (4, 6), 6: (6, 7), 7: (7, 8)}
-
-        for s in range(NS + 6):
-            for kind, idx in later_loads.get(s, []):
-                if kind == "w3":
-                    load_w3(idx, 0)
-                    load_w3(idx, 1)
-                elif kind == "w4":
-                    load_w4(idx)
-                else:
-                    load_x_two(idx)
-            for e in range(E):
-                if x_t_step[e] == s:
-                    x_transposes(e)
-            if s == 2:
-                b3_transpose()
-            if 0 <= s - 1 < NS:
-                w3_quantise(s - 1)
-            if s < NS:
-                w3_regroup(s, 1, "S")
-            if 0 <= s - 3 < NS:
-                h3_regroup(s - 3)
-            if s < NS:
-                w3_regroup(s, 0, "V")
-            if s == 2:
-                b3_copy()
-            for e in range(E):
-                if x_q_step[e] == s:
-                    x_quantise(e)
-            if 0 <= s - 1 < NS:
-                stage1(s - 1)
-            if 0 <= s - 2 < NS:
-                swish(s - 2)
-            for e in range(E):
-                if x_t_step[e] == s:
-                    x_copies(e)
-            if 0 <= s - 3 < NS:
-                h3_quantise(s - 3)
-                if (s - 3) % 2 == 1:
-                    stage2((s - 3) // 2)
-            if s == 3:
-                b4_spread()
-            if s % 2 == 0 and 0 <= s // 2 - 1 < E:
-                w4_regroup(s // 2 - 1)
-            if s % 2 == 1:
-                if 0 <= s // 2 - 1 < E:
-                    w4_quantise(s // 2 - 1)
-                ea = (s - 5) // 2
-                if 0 <= ea < E:
-                    add_bias(ea)
-                    if ea in stores_after:
-                        store(stores_after[ea][0], stores_after[ea][1])
+        for item in PROGRAM:
+            emit[item[0]](*item[1:])

@@ -16,49 +16,48 @@ B, E, D, H = 256, 8, 128, 1024
 FLOPS = 2 * E * B * H * (H + D)
 
 PROGRAM = (
-    ("LWP", 0, 0), ("LWP", 1, 0), ("LB3",), ("LB4",), ("LX1", 0), ("R", 0, 0, "V"),
-    ("LWP", 0, 1), ("R", 0, 1, "V"), ("LWP", 1, 1), ("B3A",), ("Q", 0), ("XT", 0),
-    ("LW", 1, 0), ("B3T",), ("R", 1, 0, "V"), ("XC", 0, 0, "S"), ("XC", 0, 1, "S"), ("B3C",),
-    ("LX1", 1), ("R", 1, 1, "V"), ("B4M", 0), ("B4M", 1), ("B4C", 1, "S"), ("XQ", 0),
-    ("LW", 1, 1), ("B4M", 3), ("B4C", 0, "V"), ("B4C", 3, "S"), ("Q", 1), ("R", 2, 0, "S"),
-    ("M", 0, 0), ("B4M", 2), ("R", 3, 0, "V"), ("M", 0, 1), ("LX2", 1), ("XT", 1),
-    ("B4C", 2, "V"), ("A", 0, 0), ("A", 0, 1), ("M", 1, 0), ("XC", 1, 0, "S"), ("R", 2, 1, "V"),
-    ("LW4", 0), ("M", 1, 1), ("XC", 1, 1, "S"), ("R", 3, 1, "S"), ("Q", 2), ("LW", 2, 0),
-    ("XQ", 1), ("XT", 2), ("H", 0), ("A", 1, 0), ("LW", 2, 1), ("W4R", 0),
-    ("M", 2, 0), ("XC", 2, 0, "S"), ("Q", 3), ("M", 2, 1), ("XC", 2, 1, "S"), ("A", 1, 1),
-    ("XT", 3), ("XQ", 2), ("A", 2, 0), ("LW4", 1), ("H", 1), ("R", 4, 0, "S"),
-    ("M", 3, 0), ("HQ", 0), ("W4Q", 0), ("LW", 3, 0), ("HQ", 1), ("M", 3, 1),
-    ("R", 5, 0, "V"), ("O", 0), ("R", 4, 1, "S"), ("R", 5, 1, "V"), ("LW", 3, 1), ("ADD", 0),
-    ("W4R", 1), ("A", 2, 1), ("Q", 5), ("XC", 3, 0, "S"), ("LW4", 2), ("R", 6, 0, "S"),
-    ("Q", 4), ("LX2", 2), ("H", 2), ("M", 4, 0), ("HQ", 2), ("R", 6, 1, "S"),
-    ("W4Q", 1), ("R", 7, 0, "V"), ("M", 4, 1), ("LW", 4, 0), ("W4R", 2), ("R", 7, 1, "V"),
-    ("XC", 3, 1, "S"), ("A", 3, 0), ("LW", 4, 1), ("XT", 4), ("XQ", 3), ("A", 3, 1),
-    ("Q", 6), ("A", 4, 0), ("M", 5, 0), ("A", 4, 1), ("H", 3), ("M", 5, 1),
-    ("XC", 4, 0, "S"), ("LW4", 3), ("H", 4), ("R", 8, 0, "S"), ("M", 6, 0), ("Q", 7),
-    ("LW", 5, 0), ("M", 6, 1), ("HQ", 3), ("HQ", 4), ("R", 8, 1, "S"), ("W4Q", 2),
-    ("O", 1), ("R", 9, 0, "V"), ("LW", 5, 1), ("ADD", 1), ("W4R", 3), ("XC", 4, 1, "S"),
-    ("Q", 8), ("A", 5, 0), ("XT", 5), ("LW4", 4), ("A", 5, 1), ("XQ", 4),
-    ("R", 9, 1, "S"), ("LX2", 3), ("M", 7, 0), ("H", 5), ("HQ", 5), ("M", 7, 1),
-    ("W4Q", 3), ("R", 10, 0, "V"), ("O", 2), ("A", 6, 0), ("LW", 6, 0), ("Q", 9),
-    ("A", 6, 1), ("M", 8, 0), ("R", 10, 1, "S"), ("ADD", 2), ("M", 8, 1), ("H", 6),
-    ("LW", 6, 1), ("W4R", 4), ("HQ", 6), ("XC", 5, 0, "S"), ("R", 11, 0, "V"), ("XC", 5, 1, "S"),
-    ("A", 7, 0), ("Q", 10), ("XT", 6), ("LW4", 5), ("A", 7, 1), ("R", 11, 1, "S"),
-    ("XQ", 5), ("M", 9, 0), ("LW", 7, 0), ("H", 7), ("M", 9, 1), ("HQ", 7),
-    ("W4Q", 4), ("R", 12, 0, "V"), ("O", 3), ("A", 8, 0), ("LW", 7, 1), ("A", 8, 1),
-    ("M", 10, 0), ("ADD", 3), ("R", 12, 1, "S"), ("Q", 11), ("M", 10, 1), ("H", 8),
-    ("LW4", 6), ("W4R", 5), ("XC", 6, 0, "S"), ("LW4", 7), ("Q", 12), ("XC", 6, 1, "S"),
-    ("A", 9, 0), ("ST", 0, 4), ("XT", 7), ("XQ", 6), ("A", 9, 1), ("HQ", 8),
-    ("R", 13, 0, "V"), ("R", 13, 1, "S"), ("M", 11, 0), ("M", 11, 1), ("H", 9), ("W4R", 6),
-    ("A", 10, 0), ("HQ", 9), ("Q", 13), ("A", 10, 1), ("M", 12, 0), ("R", 14, 0, "S"),
-    ("H", 10), ("O", 4), ("HQ", 10), ("M", 12, 1), ("ADD", 4), ("W4Q", 5),
-    ("R", 14, 1, "V"), ("XC", 7, 0, "S"), ("XC", 7, 1, "S"), ("Q", 14), ("A", 11, 0), ("A", 11, 1),
-    ("M", 13, 0), ("XQ", 7), ("R", 15, 0, "S"), ("H", 11), ("M", 13, 1), ("W4R", 7),
-    ("HQ", 11), ("R", 15, 1, "V"), ("A", 12, 0), ("O", 5), ("A", 12, 1), ("M", 14, 0),
-    ("Q", 15), ("A", 13, 0), ("M", 14, 1), ("A", 13, 1), ("ADD", 5), ("H", 12),
-    ("A", 14, 0), ("M", 15, 0), ("ST", 4, 6), ("H", 13), ("A", 14, 1), ("M", 15, 1),
-    ("HQ", 12), ("A", 15, 0), ("W4Q", 6), ("H", 14), ("A", 15, 1), ("HQ", 13),
-    ("HQ", 14), ("H", 15), ("O", 6), ("W4Q", 7), ("HQ", 15), ("ADD", 6),
-    ("O", 7), ("ST", 6, 7), ("ADD", 7), ("ST", 7, 8),
+    ("LB3",), ("LX1", 0), ("LWQ", 0, 0), ("LWQ", 1, 0), ("LWQ", 0, 1), ("XT", 0),
+    ("LWQ", 1, 1), ("RQ", 0, 0, "S"), ("LX1", 1), ("XC", 0, 1, "S"), ("LWP", 0, 1), ("RQ", 0, 1, "V"),
+    ("XC", 0, 0, "S"), ("RQ", 1, 0, "S"), ("RQ", 1, 1, "V"), ("LWP", 1, 1), ("B3A",), ("XQ", 0),
+    ("XT", 1), ("Q", 0), ("LW", 1, 0), ("B3T",), ("XC", 1, 1, "S"), ("R", 1, 0, "V"),
+    ("M", 0, 0), ("B3C",), ("M", 0, 1), ("R", 1, 1, "V"), ("A", 0, 0), ("LW", 1, 1),
+    ("XC", 1, 0, "S"), ("Q", 1), ("A", 0, 1), ("H", 0, "S"), ("R", 3, 0, "V"), ("LX2", 1),
+    ("M", 1, 0), ("R", 2, 0, "V"), ("M", 1, 1), ("A", 1, 0), ("R", 3, 1, "V"), ("R", 2, 1, "S"),
+    ("LW", 2, 0), ("HQ", 0), ("XQ", 1), ("A", 1, 1), ("Q", 2), ("XT", 2),
+    ("LW", 2, 1), ("H", 1, "S"), ("Q", 3), ("M", 2, 1), ("XC", 2, 0, "S"), ("XC", 2, 1, "S"),
+    ("HQ", 1), ("M", 2, 0), ("LW", 3, 0), ("R", 5, 0, "V"), ("A", 2, 1), ("XT", 3),
+    ("A", 2, 0), ("XQ", 2), ("R", 4, 0, "V"), ("M", 3, 0), ("R", 4, 1, "S"), ("LW4", 0),
+    ("M", 3, 1), ("R", 5, 1, "V"), ("LW", 3, 1), ("Q", 5), ("A", 3, 0), ("XC", 3, 1, "S"),
+    ("Q", 4), ("A", 3, 1), ("LW", 4, 0), ("XC", 3, 0, "S"), ("W4R", 0, "V"), ("H", 2, "S"),
+    ("M", 4, 0), ("W4Q", 0), ("H", 3, "V"), ("M", 5, 1), ("R", 6, 0, "S"), ("LX2", 2),
+    ("R", 7, 1, "V"), ("M", 4, 1), ("XQ", 3), ("M", 5, 0), ("HQ", 2), ("R", 7, 0, "V"),
+    ("R", 8, 0, "S"), ("LW", 4, 1), ("O", 0), ("HQ", 3), ("R", 6, 1, "V"), ("A", 5, 0),
+    ("XT", 4), ("Q", 6), ("LW", 5, 0), ("A", 5, 1), ("A", 4, 0), ("Q", 7),
+    ("XC", 4, 1, "S"), ("LW4", 1), ("XC", 4, 0, "S"), ("R", 8, 1, "V"), ("M", 7, 1), ("A", 4, 1),
+    ("LW", 5, 1), ("R", 9, 1, "V"), ("R", 9, 0, "S"), ("M", 6, 0), ("XT", 5), ("H", 4, "V"),
+    ("R", 10, 0, "V"), ("M", 6, 1), ("LW4", 3), ("W4R", 1, "S"), ("H", 5, "V"), ("M", 7, 0),
+    ("LB4",), ("Q", 8), ("A", 6, 0), ("XC", 5, 1, "S"), ("XQ", 4), ("XC", 5, 0, "S"),
+    ("HQ", 5), ("A", 6, 1), ("LW", 6, 0), ("R", 11, 0, "V"), ("M", 8, 0), ("A", 7, 0),
+    ("M", 8, 1), ("R", 10, 1, "S"), ("HQ", 4), ("Q", 9), ("LW4", 2), ("W4R", 3, "V"),
+    ("M", 9, 0), ("ADD", 0), ("LW", 6, 1), ("A", 8, 1), ("R", 11, 1, "V"), ("A", 7, 1),
+    ("H", 6, "S"), ("W4Q", 1), ("M", 9, 1), ("Q", 10), ("LW4", 4), ("O", 1),
+    ("A", 8, 0), ("W4Q", 3), ("A", 9, 1), ("XQ", 5), ("LX2", 3), ("Q", 11),
+    ("H", 8, "S"), ("M", 10, 1), ("R", 13, 1, "S"), ("W4R", 2, "V"), ("M", 11, 1), ("W4Q", 2),
+    ("LW", 7, 0), ("ADD", 1), ("R", 12, 1, "V"), ("O", 2), ("M", 10, 0), ("R", 13, 0, "S"),
+    ("H", 7, "V"), ("W4R", 4, "V"), ("XT", 6), ("LW4", 5), ("HQ", 6), ("R", 12, 0, "V"),
+    ("LW", 7, 1), ("A", 10, 0), ("ADD", 2), ("A", 9, 0), ("HQ", 7), ("Q", 13),
+    ("XC", 6, 0, "S"), ("O", 3), ("XC", 6, 1, "S"), ("M", 11, 0), ("Q", 12), ("A", 10, 1),
+    ("XT", 7), ("R", 14, 0, "S"), ("H", 9, "V"), ("W4Q", 4), ("XQ", 6), ("HQ", 9),
+    ("A", 11, 0), ("ADD", 3), ("M", 12, 1), ("HQ", 8), ("ST", 0, 4), ("XC", 7, 1, "S"),
+    ("W4R", 5, "V"), ("M", 12, 0), ("A", 11, 1), ("R", 14, 1, "V"), ("XC", 7, 0, "S"), ("O", 4),
+    ("LW4", 6), ("A", 12, 0), ("Q", 14), ("M", 13, 0), ("H", 11, "S"), ("LW4", 7),
+    ("M", 13, 1), ("XQ", 7), ("R", 15, 0, "V"), ("A", 12, 1), ("M", 14, 0), ("H", 10, "S"),
+    ("R", 15, 1, "V"), ("M", 14, 1), ("A", 13, 0), ("Q", 15), ("A", 14, 0), ("A", 13, 1),
+    ("HQ", 10), ("H", 12, "V"), ("A", 14, 1), ("M", 15, 0), ("W4Q", 5), ("H", 13, "S"),
+    ("HQ", 12), ("M", 15, 1), ("W4R", 7, "V"), ("HQ", 11), ("A", 15, 1), ("ADD", 4),
+    ("W4R", 6, "V"), ("A", 15, 0), ("O", 5), ("W4Q", 6), ("H", 14, "S"), ("HQ", 13),
+    ("ADD", 5), ("W4Q", 7), ("O", 6), ("ST", 4, 6), ("H", 15, "V"), ("HQ", 15),
+    ("HQ", 14), ("ADD", 6), ("O", 7), ("ST", 6, 7), ("ADD", 7), ("ST", 7, 8),
 )
 
 
@@ -77,11 +76,12 @@ def tile_environvectorfield_pb_kernel(tc, h2, W3, b3, W4, b4, out):
     w3rows = W3.rearrange("e (g p j) n -> e g p j n", g=2, p=P, j=4)
     w4v = W4.rearrange("e (a p) d -> e p a d", p=P)
     b3v = b3.rearrange("e (j q) -> (e j) q", q=P)
-    b4v = b4.rearrange("(o e) d -> o (e d)", o=1)
+    b4v = b4.rearrange("e d -> (e d)").partition_broadcast(P)
     outv = out.rearrange("(p bt e) d -> p bt (e d)", bt=2, e=E)
 
     with ExitStack() as ctx:
         const = ctx.enter_context(tc.tile_pool(name="const", bufs=1))
+        raw0 = ctx.enter_context(tc.tile_pool(name="raw0", bufs=1))
         rawp = ctx.enter_context(tc.tile_pool(name="rawp", bufs=8))
         grpp = ctx.enter_context(tc.tile_pool(name="grpp", bufs=3))
         w3q = ctx.enter_context(tc.tile_pool(name="w3q", bufs=3))
@@ -105,12 +105,20 @@ def tile_environvectorfield_pb_kernel(tc, h2, W3, b3, W4, b4, out):
                 nc.scalar.copy(out=dst, in_=src)
 
         def load_w3_piece(g, h):
-            raw = rawp.tile([P, 2048], BF16, name="raw", tag="raw")
+            raw = raw0.tile([P, 2048], BF16, name="rawh%d" % g, tag="rawh%d" % g)
             nc.sync.dma_start(
                 out=raw[:].rearrange("p (j n) -> p j n", j=4),
                 in_=w3rows[0, g][:, :, 512 * h : 512 * h + 512],
             )
             st[("raw", 0, g, h)] = raw[:].rearrange("p (j n) -> p j n", j=4)
+
+        def load_w3_quarter(g, q):
+            raw = raw0.tile([P, 1024], BF16, name="rawq%d%d" % (g, q), tag="rawq%d%d" % (g, q))
+            nc.sync.dma_start(
+                out=raw[:].rearrange("p (j n) -> p j n", j=4),
+                in_=w3rows[0, g][:, :, 256 * q : 256 * q + 256],
+            )
+            st[("rawq", g, q)] = raw[:].rearrange("p (j n) -> p j n", j=4)
 
         def load_w3(e, g):
             raw = rawp.tile([P, 4096], BF16, name="raw", tag="raw")
@@ -143,7 +151,7 @@ def tile_environvectorfield_pb_kernel(tc, h2, W3, b3, W4, b4, out):
             nc.sync.dma_start(out=b3row[0:64, :], in_=b3v)
 
         def load_b4():
-            nc.sync.dma_start(out=b4z[0:1, :], in_=b4v)
+            nc.sync.dma_start(out=b4bc[:], in_=b4v)
 
         def x_transposes(e):
             x32 = st[("x", e // 2)][:].bitcast(F32)
@@ -182,6 +190,14 @@ def tile_environvectorfield_pb_kernel(tc, h2, W3, b3, W4, b4, out):
                 st[("grp", s)] = grp_new
             grp = st[("grp", s)]
             dst, src = regroup_views(grp[:, 2048 * g : 2048 * g + 2048], st[("raw", s // 2, g, s % 2)])
+            copy_on(engine, dst, src)
+
+        def w3_regroup_quarter(g, q, engine):
+            if ("grp", 0) not in st:
+                grp_new = grpp.tile([P, 4096], BF16, name="grp", tag="grp", align_bytes=64)
+                st[("grp", 0)] = grp_new
+            lo = 2048 * g + 1024 * q
+            dst, src = regroup_views(st[("grp", 0)][:, lo : lo + 1024], st[("rawq", g, q)])
             copy_on(engine, dst, src)
 
         def w3_quantise(s):
@@ -225,10 +241,10 @@ def tile_environvectorfield_pb_kernel(tc, h2, W3, b3, W4, b4, out):
                     scale=1.0,
                 )
 
-        def h3_regroup(s):
+        def h3_regroup(s, engine):
             g3 = h3p.tile([P, 1024], BF16, name="g3", tag="g3", align_bytes=64)
             dst, src = regroup_views(g3[:], st[("a3", s)][:].rearrange("p (t b) -> p t b", t=4))
-            nc.vector.tensor_copy(out=dst, in_=src)
+            copy_on(engine, dst, src)
             st[("g3", s)] = g3
 
         def h3_quantise(s):
@@ -244,15 +260,21 @@ def tile_environvectorfield_pb_kernel(tc, h2, W3, b3, W4, b4, out):
                 in_=st[("g3", s)][:],
             )
 
-        def w4_regroup(e):
+        def w4_regroup(e, engine):
             w4raw = st[("w4raw", e)]
             w4g = w4q.tile([P, 1024], BF16, name="w4g", tag="w4g", align_bytes=64)
-            for g in range(2):
-                dst, src = regroup_views(
-                    w4g[:, 512 * g : 512 * g + 512],
-                    w4raw[:, 512 * g : 512 * g + 512].rearrange("p (t d) -> p t d", t=4),
+            if engine == "V":
+                nc.vector.tensor_copy(
+                    out=w4g[:].rearrange("p (g c i t) -> p g c t i", g=2, i=4, t=4),
+                    in_=w4raw[:].rearrange("p (g t c i) -> p g c t i", g=2, t=4, i=4),
                 )
-                nc.vector.tensor_copy(out=dst, in_=src)
+            else:
+                for g in range(2):
+                    dst, src = regroup_views(
+                        w4g[:, 512 * g : 512 * g + 512],
+                        w4raw[:, 512 * g : 512 * g + 512].rearrange("p (t d) -> p t d", t=4),
+                    )
+                    nc.scalar.copy(out=dst, in_=src)
             st[("w4g", e)] = w4g
 
         def w4_quantise(e):
@@ -304,27 +326,15 @@ def tile_environvectorfield_pb_kernel(tc, h2, W3, b3, W4, b4, out):
         def b3_copy():
             nc.vector.tensor_copy(out=b3T[:], in_=st["b3ps"][:, 0:64])
 
-        def b4_matmul(c):
-            b4ps = ps2.tile([P, 256], F32, name="b4ps", tag="acc2")
-            nc.tensor.matmul(b4ps[:], lhsT=ones[:], rhs=b4z[:, 256 * c : 256 * c + 256], start=True, stop=True)
-            st[("b4ps", c)] = b4ps
-
-        def b4_copy(c, engine):
-            copy_on(engine, b4bc[:, 256 * c : 256 * c + 256], st[("b4ps", c)][:])
-
-        b4z = const.tile([P, E * D], BF16)
-        nc.gpsimd.memset(b4z[:].bitcast(F32), 0.0)
         b3row = const.tile([P, P], BF16)
         nc.gpsimd.memset(b3row[:].bitcast(F32), 0.0)
         ident = const.tile([P, P], F32)
         make_identity(nc, ident[:])
-        ones = const.tile([P, P], BF16)
-        nc.vector.memset(ones[:], 1.0)
         warm = const.tile([P, 1], F32)
         nc.vector.memset(warm[:], 0.0)
         warm2 = const.tile([P, 1], F32)
         nc.scalar.activation(out=warm2[:], in_=warm[:], func=ACT.Silu)
-        b4bc = const.tile([P, E * D], F32)
+        b4bc = const.tile([P, E * D], BF16)
         b3f = const.tile([P, P], F32)
         b3T = const.tile([P, 64], F32)
         out_sb = const.tile([P, 2 * E * D], F32)
@@ -335,7 +345,7 @@ def tile_environvectorfield_pb_kernel(tc, h2, W3, b3, W4, b4, out):
             "LB3": load_b3, "LB4": load_b4, "XT": x_transposes, "XC": x_copy, "XQ": x_quantise,
             "R": w3_regroup, "Q": w3_quantise, "M": stage1, "A": swish, "H": h3_regroup, "HQ": h3_quantise,
             "W4R": w4_regroup, "W4Q": w4_quantise, "O": stage2, "ADD": add_bias, "ST": store,
-            "B3A": b3_cast, "B3T": b3_transpose, "B3C": b3_copy, "B4M": b4_matmul, "B4C": b4_copy,
+            "B3A": b3_cast, "B3T": b3_transpose, "B3C": b3_copy, "LWQ": load_w3_quarter, "RQ": w3_regroup_quarter,
         }
         for item in PROGRAM:
             emit[item[0]](*item[1:])

@@ -12,340 +12,295 @@ ACT = mybir.ActivationFunctionType
 ALU = mybir.AluOpType
 
 P = 128
+PACK = 4
 B, E, D, H = 256, 8, 128, 1024
+HALVES = 2 * E
+HALF = H // 2
 FLOPS = 2 * E * B * H * (H + D)
 
-PROGRAM = (
-    ("LB3",), ("LX1", 0), ("LWQ", 0, 0), ("LWQ", 1, 0), ("LWQ", 0, 1), ("XT", 0),
-    ("LWQ", 1, 1), ("RQ", 0, 0, "S"), ("LX1", 1), ("XC", 0, 1, "S"), ("LWP", 0, 1), ("RQ", 0, 1, "V"),
-    ("XC", 0, 0, "S"), ("RQ", 1, 0, "S"), ("RQ", 1, 1, "V"), ("LWP", 1, 1), ("B3A",), ("XQ", 0),
-    ("XT", 1), ("Q", 0), ("LW", 1, 0), ("B3T",), ("XC", 1, 1, "S"), ("R", 1, 0, "V"),
-    ("M", 0, 0), ("B3C",), ("M", 0, 1), ("R", 1, 1, "V"), ("A", 0, 0), ("LW", 1, 1),
-    ("XC", 1, 0, "S"), ("Q", 1), ("A", 0, 1), ("H", 0, "S"), ("R", 3, 0, "V"), ("LX2", 1),
-    ("M", 1, 0), ("R", 2, 0, "V"), ("M", 1, 1), ("A", 1, 0), ("R", 3, 1, "V"), ("R", 2, 1, "S"),
-    ("LW", 2, 0), ("HQ", 0), ("XQ", 1), ("A", 1, 1), ("Q", 2), ("XT", 2),
-    ("LW", 2, 1), ("H", 1, "S"), ("Q", 3), ("M", 2, 1), ("XC", 2, 0, "S"), ("XC", 2, 1, "S"),
-    ("HQ", 1), ("M", 2, 0), ("LW", 3, 0), ("R", 5, 0, "V"), ("A", 2, 1), ("XT", 3),
-    ("A", 2, 0), ("XQ", 2), ("R", 4, 0, "V"), ("M", 3, 0), ("R", 4, 1, "S"), ("LW4", 0),
-    ("M", 3, 1), ("R", 5, 1, "V"), ("LW", 3, 1), ("Q", 5), ("A", 3, 0), ("XC", 3, 1, "S"),
-    ("Q", 4), ("A", 3, 1), ("LW", 4, 0), ("XC", 3, 0, "S"), ("W4R", 0, "V"), ("H", 2, "S"),
-    ("M", 4, 0), ("W4Q", 0), ("H", 3, "V"), ("M", 5, 1), ("R", 6, 0, "S"), ("LX2", 2),
-    ("R", 7, 1, "V"), ("M", 4, 1), ("XQ", 3), ("M", 5, 0), ("HQ", 2), ("R", 7, 0, "V"),
-    ("R", 8, 0, "S"), ("LW", 4, 1), ("O", 0), ("HQ", 3), ("R", 6, 1, "V"), ("A", 5, 0),
-    ("XT", 4), ("Q", 6), ("LW", 5, 0), ("A", 5, 1), ("A", 4, 0), ("Q", 7),
-    ("XC", 4, 1, "S"), ("LW4", 1), ("XC", 4, 0, "S"), ("R", 8, 1, "V"), ("M", 7, 1), ("A", 4, 1),
-    ("LW", 5, 1), ("R", 9, 1, "V"), ("R", 9, 0, "S"), ("M", 6, 0), ("XT", 5), ("H", 4, "V"),
-    ("R", 10, 0, "V"), ("M", 6, 1), ("LW4", 3), ("W4R", 1, "S"), ("H", 5, "V"), ("M", 7, 0),
-    ("LB4",), ("Q", 8), ("A", 6, 0), ("XC", 5, 1, "S"), ("XQ", 4), ("XC", 5, 0, "S"),
-    ("HQ", 5), ("A", 6, 1), ("LW", 6, 0), ("R", 11, 0, "V"), ("M", 8, 0), ("A", 7, 0),
-    ("M", 8, 1), ("R", 10, 1, "S"), ("HQ", 4), ("Q", 9), ("LW4", 2), ("W4R", 3, "V"),
-    ("M", 9, 0), ("ADD", 0), ("LW", 6, 1), ("A", 8, 1), ("R", 11, 1, "V"), ("A", 7, 1),
-    ("H", 6, "S"), ("W4Q", 1), ("M", 9, 1), ("Q", 10), ("LW4", 4), ("O", 1),
-    ("A", 8, 0), ("W4Q", 3), ("A", 9, 1), ("XQ", 5), ("LX2", 3), ("Q", 11),
-    ("H", 8, "S"), ("M", 10, 1), ("R", 13, 1, "S"), ("W4R", 2, "V"), ("M", 11, 1), ("W4Q", 2),
-    ("LW", 7, 0), ("ADD", 1), ("R", 12, 1, "V"), ("O", 2), ("M", 10, 0), ("R", 13, 0, "S"),
-    ("H", 7, "V"), ("W4R", 4, "V"), ("XT", 6), ("LW4", 5), ("HQ", 6), ("R", 12, 0, "V"),
-    ("LW", 7, 1), ("A", 10, 0), ("ADD", 2), ("A", 9, 0), ("HQ", 7), ("Q", 13),
-    ("XC", 6, 0, "S"), ("O", 3), ("XC", 6, 1, "S"), ("M", 11, 0), ("Q", 12), ("A", 10, 1),
-    ("XT", 7), ("R", 14, 0, "S"), ("H", 9, "V"), ("W4Q", 4), ("XQ", 6), ("HQ", 9),
-    ("A", 11, 0), ("ADD", 3), ("M", 12, 1), ("HQ", 8), ("ST", 0, 4), ("XC", 7, 1, "S"),
-    ("W4R", 5, "V"), ("M", 12, 0), ("A", 11, 1), ("R", 14, 1, "V"), ("XC", 7, 0, "S"), ("O", 4),
-    ("LW4", 6), ("A", 12, 0), ("Q", 14), ("M", 13, 0), ("H", 11, "S"), ("LW4", 7),
-    ("M", 13, 1), ("XQ", 7), ("R", 15, 0, "V"), ("A", 12, 1), ("M", 14, 0), ("H", 10, "S"),
-    ("R", 15, 1, "V"), ("M", 14, 1), ("A", 13, 0), ("Q", 15), ("A", 14, 0), ("A", 13, 1),
-    ("HQ", 10), ("H", 12, "V"), ("A", 14, 1), ("M", 15, 0), ("W4Q", 5), ("H", 13, "S"),
-    ("HQ", 12), ("M", 15, 1), ("W4R", 7, "V"), ("HQ", 11), ("A", 15, 1), ("ADD", 4),
-    ("W4R", 6, "V"), ("A", 15, 0), ("O", 5), ("W4Q", 6), ("H", 14, "S"), ("HQ", 13),
-    ("ADD", 5), ("W4Q", 7), ("O", 6), ("ST", 4, 6), ("H", 15, "V"), ("HQ", 15),
-    ("HQ", 14), ("ADD", 6), ("O", 7), ("ST", 6, 7), ("ADD", 7), ("ST", 7, 8),
-)
+W3_LOAD_AFTER_STEP = {0: 3, 1: 4, 3: 5, 5: 6, 7: 7}
+STORE_AFTER = {3: 0, 5: 4, 6: 6, 7: 7}
 
 
-def regroup_views(dst, src):
+def regroup_views(grouped, planes):
     return (
-        dst.rearrange("p (c i t) -> p c t i", i=4, t=4),
-        src.rearrange("p t (c i) -> p c t i", i=4),
+        grouped.rearrange("p (c i t) -> p c t i", i=4, t=PACK),
+        planes.rearrange("p t (c i) -> p c t i", i=4),
     )
 
 
 def tile_environvectorfield_pb_kernel(tc, h2, W3, b3, W4, b4, out):
     nc = tc.nc
-    h2one = h2.rearrange("(p bt) e k -> e p bt k", bt=2)
-    h2two = h2.rearrange("(p bt) (q f) k -> q p bt (f k)", bt=2, f=2)
-    w3whole = W3.rearrange("e (g p j) n -> e g p (j n)", g=2, p=P, j=4)
-    w3rows = W3.rearrange("e (g p j) n -> e g p j n", g=2, p=P, j=4)
-    w4v = W4.rearrange("e (a p) d -> e p a d", p=P)
-    b3v = b3.rearrange("e (j q) -> (e j) q", q=P)
-    b4v = b4.rearrange("e d -> (e d)").partition_broadcast(P)
-    outv = out.rearrange("(p bt e) d -> p bt (e d)", bt=2, e=E)
+    h2_view = h2.rearrange("(p i) e k -> e p i k", i=2)
+    w3_tiles = W3.rearrange("e (g p t) n -> e g p (t n)", g=2, p=P, t=PACK)
+    w3_planes = W3.rearrange("e (g p t) n -> e g p t n", g=2, p=P, t=PACK)
+    w4_view = W4.rearrange("e (a p) d -> e p a d", p=P)
+    b3_rows = b3.rearrange("e (j q) -> (e j) q", q=P)
+    b4_row = b4.rearrange("(o e) d -> o (e d)", o=1)
+    out_view = out.rearrange("(p i e) d -> p i (e d)", i=2, e=E)
 
     with ExitStack() as ctx:
         const = ctx.enter_context(tc.tile_pool(name="const", bufs=1))
-        raw0 = ctx.enter_context(tc.tile_pool(name="raw0", bufs=1))
-        rawp = ctx.enter_context(tc.tile_pool(name="rawp", bufs=8))
-        grpp = ctx.enter_context(tc.tile_pool(name="grpp", bufs=3))
-        w3q = ctx.enter_context(tc.tile_pool(name="w3q", bufs=3))
-        xp = ctx.enter_context(tc.tile_pool(name="xp", bufs=4))
-        xq = ctx.enter_context(tc.tile_pool(name="xq", bufs=2))
-        h3p = ctx.enter_context(tc.tile_pool(name="h3p", bufs=3))
-        h3q = ctx.enter_context(tc.tile_pool(name="h3q", bufs=2))
-        w4p = ctx.enter_context(tc.tile_pool(name="w4p", bufs=8))
-        w4q = ctx.enter_context(tc.tile_pool(name="w4q", bufs=3))
-        psx = ctx.enter_context(tc.psum_pool(name="psx", bufs=2))
-        ps1 = ctx.enter_context(tc.psum_pool(name="ps1", bufs=4))
-        ps2 = ctx.enter_context(tc.psum_pool(name="ps2", bufs=2))
+        w3_in = ctx.enter_context(tc.tile_pool(name="w3_in", bufs=8))
+        h2_in = ctx.enter_context(tc.tile_pool(name="h2_in", bufs=E))
+        w4_in = ctx.enter_context(tc.tile_pool(name="w4_in", bufs=E))
+        three = ctx.enter_context(tc.tile_pool(name="three", bufs=3))
+        two = ctx.enter_context(tc.tile_pool(name="two", bufs=2))
+        ps_h2 = ctx.enter_context(tc.psum_pool(name="ps_h2", bufs=2))
+        ps_first = ctx.enter_context(tc.psum_pool(name="ps_first", bufs=4))
+        ps_second = ctx.enter_context(tc.psum_pool(name="ps_second", bufs=2))
         ctx.enter_context(tc.manual_schedule())
 
-        st = {}
-
-        def copy_on(engine, dst, src):
-            if engine == "V":
-                nc.vector.tensor_copy(out=dst, in_=src)
-            else:
-                nc.scalar.copy(out=dst, in_=src)
+        live = {}
 
         def load_w3_piece(g, h):
-            raw = raw0.tile([P, 2048], BF16, name="rawh%d" % g, tag="rawh%d" % g)
-            nc.sync.dma_start(
-                out=raw[:].rearrange("p (j n) -> p j n", j=4),
-                in_=w3rows[0, g][:, :, 512 * h : 512 * h + 512],
-            )
-            st[("raw", 0, g, h)] = raw[:].rearrange("p (j n) -> p j n", j=4)
-
-        def load_w3_quarter(g, q):
-            raw = raw0.tile([P, 1024], BF16, name="rawq%d%d" % (g, q), tag="rawq%d%d" % (g, q))
-            nc.sync.dma_start(
-                out=raw[:].rearrange("p (j n) -> p j n", j=4),
-                in_=w3rows[0, g][:, :, 256 * q : 256 * q + 256],
-            )
-            st[("rawq", g, q)] = raw[:].rearrange("p (j n) -> p j n", j=4)
+            w3_raw = w3_in.tile([P, PACK * HALF], BF16, name="w3_raw", tag="w3_raw")
+            planes = w3_raw[:].rearrange("p (t n) -> p t n", t=PACK)
+            nc.sync.dma_start(out=planes, in_=w3_planes[0, g][:, :, HALF * h : HALF * (h + 1)])
+            live[("w3_raw", h, g)] = planes
 
         def load_w3(e, g):
-            raw = rawp.tile([P, 4096], BF16, name="raw", tag="raw")
-            nc.sync.dma_start(out=raw[:], in_=w3whole[e, g])
-            rows = raw[:].rearrange("p (j n) -> p j n", j=4)
+            w3_raw = w3_in.tile([P, PACK * H], BF16, name="w3_raw", tag="w3_raw")
+            nc.sync.dma_start(out=w3_raw[:], in_=w3_tiles[e, g])
+            planes = w3_raw[:].rearrange("p (t n) -> p t n", t=PACK)
             for h in range(2):
-                st[("raw", e, g, h)] = rows[:, :, 512 * h : 512 * h + 512]
+                live[("w3_raw", 2 * e + h, g)] = planes[:, :, HALF * h : HALF * (h + 1)]
 
-        def load_x_one(e):
-            if ("x", e // 2) not in st:
-                x_new = xp.tile([P, 4096], BF16, name="x_sb", tag="x_sb")
-                st[("x", e // 2)] = x_new
-            x_sb = st[("x", e // 2)]
-            nc.sync.dma_start(
-                out=x_sb[:].rearrange("p (bt f k) -> p bt f k", bt=2, f=2)[:, :, e % 2, :],
-                in_=h2one[e],
-            )
-
-        def load_x_two(q):
-            x_sb = xp.tile([P, 4096], BF16, name="x_sb", tag="x_sb")
-            st[("x", q)] = x_sb
-            nc.sync.dma_start(out=x_sb[:].rearrange("p (bt x) -> p bt x", bt=2), in_=h2two[q])
+        def load_h2(e):
+            h2_raw = h2_in.tile([P, 2 * H], BF16, name="h2_raw", tag="h2_raw")
+            nc.sync.dma_start(out=h2_raw[:].rearrange("p (i k) -> p i k", i=2), in_=h2_view[e])
+            live[("h2_raw", e)] = h2_raw
 
         def load_w4(e):
-            w4raw = w4p.tile([P, 8 * D], BF16, name="w4raw", tag="w4raw")
-            nc.sync.dma_start(out=w4raw[:].rearrange("p (a d) -> p a d", a=8), in_=w4v[e])
-            st[("w4raw", e)] = w4raw
+            w4_raw = w4_in.tile([P, 2 * PACK * D], BF16, name="w4_raw", tag="w4_raw")
+            nc.sync.dma_start(out=w4_raw[:].rearrange("p (a d) -> p a d", a=2 * PACK), in_=w4_view[e])
+            live[("w4_raw", e)] = w4_raw
 
-        def load_b3():
-            nc.sync.dma_start(out=b3row[0:64, :], in_=b3v)
+        def load_environment(e):
+            load_w3(e, 0)
+            load_h2(e)
+            load_w3(e, 1)
+            load_w4(e - 1)
 
-        def load_b4():
-            nc.sync.dma_start(out=b4bc[:], in_=b4v)
-
-        def x_transposes(e):
-            x32 = st[("x", e // 2)][:].bitcast(F32)
+        def transpose_h2(e):
+            words = live[("h2_raw", e)][:].bitcast(F32)
             for g in range(2):
-                xt = psx.tile([P, 512], F32, name="xt", tag="xt")
+                bank = ps_h2.tile([P, 2 * B], F32, name="h2_bank", tag="h2_bank")
                 for u in range(2):
-                    for bt in range(2):
-                        base = bt * 1024 + (e % 2) * 512 + 256 * g
+                    for i in range(2):
+                        first = i * (H // 2) + g * (HALF // 2)
                         nc.tensor.transpose(
-                            xt[:, u * 256 + bt * P : u * 256 + bt * P + P],
-                            x32[:, base : base + 256].rearrange("p (w u) -> p u w", u=2)[:, u, :],
-                            ident[:],
+                            bank[:, u * B + i * P : u * B + (i + 1) * P],
+                            words[:, first : first + HALF // 2].rearrange("p (w u) -> p u w", u=2)[:, u, :],
+                            identity[:],
                         )
-                st[("xt", e, g)] = xt
+                live[("h2_bank", e, g)] = bank
 
-        def x_copy(e, g, engine):
-            if ("xg", e) not in st:
-                xg_new = xq.tile([P, 2048], BF16, name="xg", tag="xg", align_bytes=64)
-                st[("xg", e)] = xg_new
-            xg32 = st[("xg", e)][:].bitcast(F32)
-            copy_on(
-                engine,
-                xg32[:, 512 * g : 512 * g + 512].rearrange("p (b u) -> p b u", u=2),
-                st[("xt", e, g)][:].rearrange("p (u b) -> p b u", u=2),
-            )
+        def copy_h2(e):
+            h2_grouped = two.tile([P, 2 * PACK * B], BF16, name="h2_grouped", tag="h2_grouped", align_bytes=64)
+            words = h2_grouped[:].bitcast(F32)
+            for g in range(2):
+                nc.scalar.copy(
+                    out=words[:, 2 * B * g : 2 * B * (g + 1)].rearrange("p (b u) -> p b u", u=2),
+                    in_=live[("h2_bank", e, g)][:].rearrange("p (u b) -> p b u", u=2),
+                )
+            live[("h2_grouped", e)] = h2_grouped
 
-        def x_quantise(e):
-            xc = xq.tile([P, 512], U32, name="xc", tag="xc", align_bytes=64)
-            xs = xq.tile([P, 512], U8, name="xs", tag="xs", align_bytes=64)
-            nc.vector.quantize_mx(out=xc[:].bitcast(FP8X4), scales=xs[:], in_=st[("xg", e)][:])
-            st[("xc", e)] = (xc, xs)
+        def quantise_h2(e):
+            codes = two.tile([P, 2 * B], U32, name="h2_codes", tag="h2_codes", align_bytes=64)
+            scales = two.tile([P, 2 * B], U8, name="h2_scales", tag="h2_scales", align_bytes=64)
+            nc.vector.quantize_mx(out=codes[:].bitcast(FP8X4), scales=scales[:], in_=live[("h2_grouped", e)][:])
+            live[("h2_mx", e)] = (codes, scales)
 
-        def w3_regroup(s, g, engine):
-            if ("grp", s) not in st:
-                grp_new = grpp.tile([P, 4096], BF16, name="grp", tag="grp", align_bytes=64)
-                st[("grp", s)] = grp_new
-            grp = st[("grp", s)]
-            dst, src = regroup_views(grp[:, 2048 * g : 2048 * g + 2048], st[("raw", s // 2, g, s % 2)])
-            copy_on(engine, dst, src)
+        def regroup_w3(s, g):
+            if g == 0:
+                w3_new = three.tile([P, 2 * PACK * HALF], BF16, name="w3_grouped", tag="w3_grouped", align_bytes=64)
+                live[("w3_grouped", s)] = w3_new
+            chunk = live[("w3_grouped", s)][:, PACK * HALF * g : PACK * HALF * (g + 1)]
+            grouped, planes = regroup_views(chunk, live[("w3_raw", s, g)])
+            if g == 0:
+                nc.scalar.copy(out=grouped, in_=planes)
+            else:
+                nc.vector.tensor_copy(out=grouped, in_=planes)
 
-        def w3_regroup_quarter(g, q, engine):
-            if ("grp", 0) not in st:
-                grp_new = grpp.tile([P, 4096], BF16, name="grp", tag="grp", align_bytes=64)
-                st[("grp", 0)] = grp_new
-            lo = 2048 * g + 1024 * q
-            dst, src = regroup_views(st[("grp", 0)][:, lo : lo + 1024], st[("rawq", g, q)])
-            copy_on(engine, dst, src)
+        def quantise_w3(s):
+            codes = three.tile([P, 2 * HALF], U32, name="w3_codes", tag="w3_codes", align_bytes=64)
+            scales = three.tile([P, 2 * HALF], U8, name="w3_scales", tag="w3_scales", align_bytes=64)
+            nc.vector.quantize_mx(out=codes[:].bitcast(FP8X4), scales=scales[:], in_=live[("w3_grouped", s)][:])
+            live[("w3_mx", s)] = (codes, scales)
 
-        def w3_quantise(s):
-            w3c = w3q.tile([P, 1024], U32, name="w3c", tag="w3c", align_bytes=64)
-            w3s = w3q.tile([P, 1024], U8, name="w3s", tag="w3s", align_bytes=64)
-            nc.vector.quantize_mx(out=w3c[:].bitcast(FP8X4), scales=w3s[:], in_=st[("grp", s)][:])
-            st[("w3c", s)] = (w3c, w3s)
+        def first_product(s):
+            w3_codes, w3_scales = live[("w3_mx", s)]
+            h2_codes, h2_scales = live[("h2_mx", s // 2)]
+            for pair in range(2):
+                bank = ps_first.tile([P, 2 * B], F32, name="h3_bank", tag="h3_bank")
+                for i in range(2):
+                    t = 2 * pair + i
+                    for g in range(2):
+                        n_cols = slice(HALF * g + P * t, HALF * g + P * (t + 1))
+                        b_cols = slice(B * g, B * (g + 1))
+                        nc.tensor.matmul_mx(
+                            out=bank[:, B * i : B * (i + 1)],
+                            lhsT=w3_codes[:, n_cols].bitcast(FP8X4),
+                            lhsT_scale=w3_scales[:, n_cols],
+                            rhs=h2_codes[:, b_cols].bitcast(FP8X4),
+                            rhs_scale=h2_scales[:, b_cols],
+                            start=(g == 0),
+                            stop=(g == 1),
+                        )
+                live[("h3_bank", s, pair)] = bank
 
-        def stage1(s, pair):
-            w3c, w3s = st[("w3c", s)]
-            xc, xs = st[("xc", s // 2)]
-            acc = ps1.tile([P, 512], F32, name="acc", tag="acc")
-            for i in range(2):
-                j = 2 * pair + i
-                for g in range(2):
-                    cols = slice(512 * g + P * j, 512 * g + P * j + P)
-                    nc.tensor.matmul_mx(
-                        out=acc[:, 256 * i : 256 * i + 256],
-                        lhsT=w3c[:, cols].bitcast(FP8X4),
-                        lhsT_scale=w3s[:, cols],
-                        rhs=xc[:, 256 * g : 256 * g + 256].bitcast(FP8X4),
-                        rhs_scale=xs[:, 256 * g : 256 * g + 256],
-                        start=(g == 0),
-                        stop=(g == 1),
-                    )
-            st[("acc", s, pair)] = acc
-
-        def swish(s, pair):
-            if ("a3", s) not in st:
-                a3_new = h3p.tile([P, 1024], BF16, name="a3", tag="a3")
-                st[("a3", s)] = a3_new
-            a3 = st[("a3", s)]
-            for i in range(2):
-                j = 2 * pair + i
-                col = 4 * s + j
+        def swish(s):
+            h3_planes = three.tile([P, PACK * B], BF16, name="h3_planes", tag="h3_planes")
+            for t in range(PACK):
                 nc.scalar.activation(
-                    out=a3[:, 256 * j : 256 * j + 256],
-                    in_=st[("acc", s, pair)][:, 256 * i : 256 * i + 256],
+                    out=h3_planes[:, B * t : B * (t + 1)],
+                    in_=live[("h3_bank", s, t // 2)][:, B * (t % 2) : B * (t % 2 + 1)],
                     func=ACT.Silu,
-                    bias=b3T[:, col : col + 1],
+                    bias=b3_cols[:, PACK * s + t : PACK * s + t + 1],
                     scale=1.0,
                 )
+            live[("h3_planes", s)] = h3_planes
 
-        def h3_regroup(s, engine):
-            g3 = h3p.tile([P, 1024], BF16, name="g3", tag="g3", align_bytes=64)
-            dst, src = regroup_views(g3[:], st[("a3", s)][:].rearrange("p (t b) -> p t b", t=4))
-            copy_on(engine, dst, src)
-            st[("g3", s)] = g3
+        def regroup_h3(s):
+            h3_grouped = three.tile([P, PACK * B], BF16, name="h3_grouped", tag="h3_grouped", align_bytes=64)
+            grouped, planes = regroup_views(
+                h3_grouped[:], live[("h3_planes", s)][:].rearrange("p (t b) -> p t b", t=PACK)
+            )
+            nc.vector.tensor_copy(out=grouped, in_=planes)
+            live[("h3_grouped", s)] = h3_grouped
 
-        def h3_quantise(s):
-            if ("h3c", s // 2) not in st:
-                h3c_new = h3q.tile([P, 512], U32, name="h3c", tag="h3c", align_bytes=64)
-                h3s_new = h3q.tile([P, 512], U8, name="h3s", tag="h3s", align_bytes=64)
-                st[("h3c", s // 2)] = (h3c_new, h3s_new)
-            h3c, h3s = st[("h3c", s // 2)]
-            h = s % 2
+        def quantise_h3(s):
+            if s % 2 == 0:
+                codes_new = two.tile([P, 2 * B], U32, name="h3_codes", tag="h3_codes", align_bytes=64)
+                scales_new = two.tile([P, 2 * B], U8, name="h3_scales", tag="h3_scales", align_bytes=64)
+                live[("h3_mx", s // 2)] = (codes_new, scales_new)
+            codes, scales = live[("h3_mx", s // 2)]
+            cols = slice(B * (s % 2), B * (s % 2 + 1))
             nc.vector.quantize_mx(
-                out=h3c[:, 256 * h : 256 * h + 256].bitcast(FP8X4),
-                scales=h3s[:, 256 * h : 256 * h + 256],
-                in_=st[("g3", s)][:],
+                out=codes[:, cols].bitcast(FP8X4), scales=scales[:, cols], in_=live[("h3_grouped", s)][:]
             )
 
-        def w4_regroup(e, engine):
-            w4raw = st[("w4raw", e)]
-            w4g = w4q.tile([P, 1024], BF16, name="w4g", tag="w4g", align_bytes=64)
-            if engine == "V":
-                nc.vector.tensor_copy(
-                    out=w4g[:].rearrange("p (g c i t) -> p g c t i", g=2, i=4, t=4),
-                    in_=w4raw[:].rearrange("p (g t c i) -> p g c t i", g=2, t=4, i=4),
+        def regroup_w4(e):
+            w4_raw = live[("w4_raw", e)]
+            w4_grouped = three.tile([P, 2 * PACK * D], BF16, name="w4_grouped", tag="w4_grouped", align_bytes=64)
+            for h in range(2):
+                cols = slice(PACK * D * h, PACK * D * (h + 1))
+                grouped, planes = regroup_views(
+                    w4_grouped[:, cols], w4_raw[:, cols].rearrange("p (t d) -> p t d", t=PACK)
                 )
-            else:
-                for g in range(2):
-                    dst, src = regroup_views(
-                        w4g[:, 512 * g : 512 * g + 512],
-                        w4raw[:, 512 * g : 512 * g + 512].rearrange("p (t d) -> p t d", t=4),
-                    )
-                    nc.scalar.copy(out=dst, in_=src)
-            st[("w4g", e)] = w4g
+                nc.vector.tensor_copy(out=grouped, in_=planes)
+            live[("w4_grouped", e)] = w4_grouped
 
-        def w4_quantise(e):
-            w4c = w4q.tile([P, 256], U32, name="w4c", tag="w4c", align_bytes=64)
-            w4s = w4q.tile([P, 256], U8, name="w4s", tag="w4s", align_bytes=64)
-            nc.vector.quantize_mx(out=w4c[:].bitcast(FP8X4), scales=w4s[:], in_=st[("w4g", e)][:])
-            st[("w4c", e)] = (w4c, w4s)
+        def quantise_w4(e):
+            codes = three.tile([P, 2 * D], U32, name="w4_codes", tag="w4_codes", align_bytes=64)
+            scales = three.tile([P, 2 * D], U8, name="w4_scales", tag="w4_scales", align_bytes=64)
+            nc.vector.quantize_mx(out=codes[:].bitcast(FP8X4), scales=scales[:], in_=live[("w4_grouped", e)][:])
+            live[("w4_mx", e)] = (codes, scales)
 
-        def stage2(e):
-            h3c, h3s = st[("h3c", e)]
-            w4c, w4s = st[("w4c", e)]
-            acc2 = ps2.tile([P, 256], F32, name="acc2", tag="acc2")
-            for bt in range(2):
-                for g in range(2):
-                    cols = slice(256 * g + P * bt, 256 * g + P * bt + P)
+        def second_product(e):
+            h3_codes, h3_scales = live[("h3_mx", e)]
+            w4_codes, w4_scales = live[("w4_mx", e)]
+            bank = ps_second.tile([P, 2 * D], F32, name="out_bank", tag="small_bank")
+            for i in range(2):
+                for h in range(2):
+                    b_cols = slice(B * h + P * i, B * h + P * (i + 1))
+                    d_cols = slice(D * h, D * (h + 1))
                     nc.tensor.matmul_mx(
-                        out=acc2[:, P * bt : P * bt + P],
-                        lhsT=h3c[:, cols].bitcast(FP8X4),
-                        lhsT_scale=h3s[:, cols],
-                        rhs=w4c[:, P * g : P * g + P].bitcast(FP8X4),
-                        rhs_scale=w4s[:, P * g : P * g + P],
-                        start=(g == 0),
-                        stop=(g == 1),
+                        out=bank[:, D * i : D * (i + 1)],
+                        lhsT=h3_codes[:, b_cols].bitcast(FP8X4),
+                        lhsT_scale=h3_scales[:, b_cols],
+                        rhs=w4_codes[:, d_cols].bitcast(FP8X4),
+                        rhs_scale=w4_scales[:, d_cols],
+                        start=(h == 0),
+                        stop=(h == 1),
                     )
-            st[("acc2", e)] = acc2
+            live[("out_bank", e)] = bank
 
-        def add_bias(e):
+        def add_b4(e):
             nc.vector.tensor_tensor(
-                out=out_v[:, :, e, :],
-                in0=st[("acc2", e)][:].rearrange("p (bt d) -> p bt d", bt=2),
-                in1=b4bc[:, D * e : D * e + D].unsqueeze(1).to_broadcast([P, 2, D]),
+                out=out_rows.rearrange("p i (e d) -> p i e d", e=E)[:, :, e, :],
+                in0=live[("out_bank", e)][:].rearrange("p (i d) -> p i d", i=2),
+                in1=b4_all[:, D * e : D * (e + 1)].unsqueeze(1).to_broadcast([P, 2, D]),
                 op=ALU.add,
             )
 
-        def store(e0, e1):
-            nc.sync.dma_start(
-                out=outv[:, :, D * e0 : D * e1],
-                in_=out_sb[:].rearrange("p (bt x) -> p bt x", bt=2)[:, :, D * e0 : D * e1],
-            )
+        def store(first, last):
+            cols = slice(D * first, D * (last + 1))
+            nc.sync.dma_start(out=out_view[:, :, cols], in_=out_rows[:, :, cols])
 
-        def b3_cast():
-            nc.vector.tensor_copy(out=b3f[:], in_=b3row[:])
+        b3_padded = const.tile([P, P], BF16)
+        nc.gpsimd.memset(b3_padded[:].bitcast(F32), 0.0)
+        b4_padded = const.tile([P, E * D], BF16)
+        nc.gpsimd.memset(b4_padded[:].bitcast(F32), 0.0)
+        identity = const.tile([P, P], F32)
+        make_identity(nc, identity[:])
+        ones = const.tile([P, P], BF16)
+        nc.vector.memset(ones[:], 1.0)
+        table_in = const.tile([P, 1], F32)
+        nc.vector.memset(table_in[:], 0.0)
+        table_out = const.tile([P, 1], F32)
+        nc.scalar.activation(out=table_out[:], in_=table_in[:], func=ACT.Silu)
 
-        def b3_transpose():
-            b3ps = ps2.tile([P, 256], F32, name="b3ps", tag="acc2")
-            nc.tensor.transpose(b3ps[:, 0:P], b3f[:], ident[:])
-            st["b3ps"] = b3ps
+        nc.sync.dma_start(out=b3_padded[0 : E * H // P, :], in_=b3_rows)
+        nc.sync.dma_start(out=b4_padded[0:1, :], in_=b4_row)
+        load_w3_piece(0, 0)
+        load_w3_piece(1, 0)
+        load_h2(0)
+        load_w3_piece(0, 1)
+        load_w3_piece(1, 1)
+        load_environment(1)
+        load_environment(2)
 
-        def b3_copy():
-            nc.vector.tensor_copy(out=b3T[:], in_=st["b3ps"][:, 0:64])
+        b3_f32 = const.tile([P, P], F32)
+        nc.vector.tensor_copy(out=b3_f32[:], in_=b3_padded[:])
+        b3_bank = ps_second.tile([P, 2 * D], F32, name="b3_bank", tag="small_bank")
+        nc.tensor.transpose(b3_bank[:, 0:P], b3_f32[:], identity[:])
+        b3_cols = const.tile([P, E * H // P], F32)
+        nc.vector.tensor_copy(out=b3_cols[:], in_=b3_bank[:, 0 : E * H // P])
+        b4_all = const.tile([P, E * D], F32)
+        for c in range(E * D // (2 * D)):
+            cols = slice(2 * D * c, 2 * D * (c + 1))
+            b4_bank = ps_second.tile([P, 2 * D], F32, name="b4_bank", tag="small_bank")
+            nc.tensor.matmul(b4_bank[:], lhsT=ones[:], rhs=b4_padded[:, cols], start=True, stop=True)
+            nc.scalar.copy(out=b4_all[:, cols], in_=b4_bank[:])
 
-        b3row = const.tile([P, P], BF16)
-        nc.gpsimd.memset(b3row[:].bitcast(F32), 0.0)
-        ident = const.tile([P, P], F32)
-        make_identity(nc, ident[:])
-        warm = const.tile([P, 1], F32)
-        nc.vector.memset(warm[:], 0.0)
-        warm2 = const.tile([P, 1], F32)
-        nc.scalar.activation(out=warm2[:], in_=warm[:], func=ACT.Silu)
-        b4bc = const.tile([P, E * D], BF16)
-        b3f = const.tile([P, P], F32)
-        b3T = const.tile([P, 64], F32)
-        out_sb = const.tile([P, 2 * E * D], F32)
-        out_v = out_sb[:].rearrange("p (bt e d) -> p bt e d", bt=2, e=E)
+        out_tile = const.tile([P, 2 * E * D], F32)
+        out_rows = out_tile[:].rearrange("p (i x) -> p i x", i=2)
 
-        emit = {
-            "LWP": load_w3_piece, "LW": load_w3, "LX1": load_x_one, "LX2": load_x_two, "LW4": load_w4,
-            "LB3": load_b3, "LB4": load_b4, "XT": x_transposes, "XC": x_copy, "XQ": x_quantise,
-            "R": w3_regroup, "Q": w3_quantise, "M": stage1, "A": swish, "H": h3_regroup, "HQ": h3_quantise,
-            "W4R": w4_regroup, "W4Q": w4_quantise, "O": stage2, "ADD": add_bias, "ST": store,
-            "B3A": b3_cast, "B3T": b3_transpose, "B3C": b3_copy, "LWQ": load_w3_quarter, "RQ": w3_regroup_quarter,
-        }
-        for item in PROGRAM:
-            emit[item[0]](*item[1:])
+        for s in range(HALVES + 4):
+            e, h = s // 2, s % 2
+            if h == 0 and e < E:
+                transpose_h2(e)
+            if 0 <= s - 1 < HALVES:
+                quantise_w3(s - 1)
+            if s < HALVES:
+                regroup_w3(s, 0)
+            if 0 <= s - 3 < HALVES:
+                regroup_h3(s - 3)
+            if s < HALVES:
+                regroup_w3(s, 1)
+            if h == 1 and e < E:
+                quantise_h2(e)
+            if 0 <= s - 1 < HALVES:
+                first_product(s - 1)
+            if 0 <= s - 2 < HALVES:
+                swish(s - 2)
+            if h == 0 and e < E:
+                copy_h2(e)
+            if h == 1 and 0 <= e - 1 < E:
+                quantise_w4(e - 1)
+            if 0 <= s - 3 < HALVES:
+                quantise_h3(s - 3)
+                if h == 0:
+                    second_product(e - 2)
+            if h == 0 and 0 <= e - 1 < E:
+                regroup_w4(e - 1)
+            if h == 1 and 0 <= e - 2 < E:
+                add_b4(e - 2)
+                if e - 2 in STORE_AFTER:
+                    store(STORE_AFTER[e - 2], e - 2)
+            if s in W3_LOAD_AFTER_STEP:
+                load_environment(W3_LOAD_AFTER_STEP[s])
+                if W3_LOAD_AFTER_STEP[s] == E - 1:
+                    load_w4(E - 1)

@@ -78,8 +78,8 @@ def tile_environvectorfield_pb_kernel(tc, h2, W3, b3, W4, b4, out):
 
         def load_environment(e):
             load_w3(e, 0)
-            load_h2(e)
             load_w3(e, 1)
+            load_h2(e)
             load_w4(e - 1)
 
         def transpose_h2(e):
@@ -182,14 +182,11 @@ def tile_environvectorfield_pb_kernel(tc, h2, W3, b3, W4, b4, out):
             )
 
         def regroup_w4(e):
-            w4_raw = live[("w4_raw", e)]
             w4_grouped = three.tile([P, 2 * PACK * D], BF16, name="w4_grouped", tag="w4_grouped", align_bytes=64)
-            for h in range(2):
-                cols = slice(PACK * D * h, PACK * D * (h + 1))
-                grouped, planes = regroup_views(
-                    w4_grouped[:, cols], w4_raw[:, cols].rearrange("p (t d) -> p t d", t=PACK)
-                )
-                nc.vector.tensor_copy(out=grouped, in_=planes)
+            nc.vector.tensor_copy(
+                out=w4_grouped[:].rearrange("p (h c i t) -> p h c t i", h=2, i=4, t=PACK),
+                in_=live[("w4_raw", e)][:].rearrange("p (h t c i) -> p h c t i", h=2, t=PACK, i=4),
+            )
             live[("w4_grouped", e)] = w4_grouped
 
         def quantise_w4(e):
@@ -288,13 +285,13 @@ def tile_environvectorfield_pb_kernel(tc, h2, W3, b3, W4, b4, out):
                 swish(s - 2)
             if h == 0 and e < E:
                 copy_h2(e)
-            if h == 1 and 0 <= e - 1 < E:
-                quantise_w4(e - 1)
+            if h == 0 and 0 <= e - 2 < E:
+                quantise_w4(e - 2)
             if 0 <= s - 3 < HALVES:
                 quantise_h3(s - 3)
                 if h == 0:
                     second_product(e - 2)
-            if h == 0 and 0 <= e - 1 < E:
+            if h == 1 and 0 <= e - 1 < E:
                 regroup_w4(e - 1)
             if h == 1 and 0 <= e - 2 < E:
                 add_b4(e - 2)

@@ -16,9 +16,11 @@ PACK = 4
 B, E, D, H = 256, 8, 128, 1024
 HALVES = 2 * E
 HALF = H // 2
+QUARTER = HALF // 2
 FLOPS = 2 * E * B * H * (H + D)
 
 W3_LOAD_AFTER_STEP = {0: 3, 1: 4, 3: 5, 5: 6, 7: 7}
+MOVED = range(2, HALVES - 2)
 STORE_AFTER = {3: 0, 5: 4, 6: 6, 7: 7}
 
 
@@ -48,7 +50,8 @@ def tile_environvectorfield_pb_kernel(tc, h2, W3, b3, W4, b4, out):
         two = ctx.enter_context(tc.tile_pool(name="two", bufs=2))
         ps_h2 = ctx.enter_context(tc.psum_pool(name="ps_h2", bufs=2))
         ps_first = ctx.enter_context(tc.psum_pool(name="ps_first", bufs=4))
-        ps_second = ctx.enter_context(tc.psum_pool(name="ps_second", bufs=2))
+        ps_second = ctx.enter_context(tc.psum_pool(name="ps_second", bufs=1))
+        ps_move = ctx.enter_context(tc.psum_pool(name="ps_move", bufs=1))
         ctx.enter_context(tc.manual_schedule())
 
         live = {}
@@ -112,12 +115,32 @@ def tile_environvectorfield_pb_kernel(tc, h2, W3, b3, W4, b4, out):
             nc.vector.quantize_mx(out=codes[:].bitcast(FP8X4), scales=scales[:], in_=live[("h2_grouped", e)][:])
             live[("h2_mx", e)] = (codes, scales)
 
+        def move_w3(s):
+            bank = ps_move.tile([P, PACK * QUARTER], BF16, name="w3_bank", tag="w3_bank")
+            by_word = live[("w3_raw", s, s % 2)].rearrange("p t n -> p n t")
+            for c in range(0, QUARTER, P):
+                nc.tensor.matmul(
+                    bank[:, PACK * c : PACK * (c + P)],
+                    lhsT=identity_bf16[:],
+                    rhs=by_word[:, QUARTER + c : QUARTER + c + P, :],
+                    start=True,
+                    stop=True,
+                )
+            live[("w3_bank", s)] = bank
+
+        def copy_moved(s):
+            first = PACK * (HALF * (s % 2) + QUARTER)
+            nc.scalar.copy(
+                out=live[("w3_grouped", s)][:, first : first + PACK * QUARTER], in_=live[("w3_bank", s)][:]
+            )
+
         def regroup_w3(s, g):
             if g == 0:
                 w3_new = three.tile([P, 2 * PACK * HALF], BF16, name="w3_grouped", tag="w3_grouped", align_bytes=64)
                 live[("w3_grouped", s)] = w3_new
-            chunk = live[("w3_grouped", s)][:, PACK * HALF * g : PACK * HALF * (g + 1)]
-            grouped, planes = regroup_views(chunk, live[("w3_raw", s, g)])
+            n = QUARTER if s in MOVED and g == s % 2 else HALF
+            chunk = live[("w3_grouped", s)][:, PACK * HALF * g : PACK * (HALF * g + n)]
+            grouped, planes = regroup_views(chunk, live[("w3_raw", s, g)][:, :, 0:n])
             if g == 0:
                 nc.scalar.copy(out=grouped, in_=planes)
             else:
@@ -232,6 +255,8 @@ def tile_environvectorfield_pb_kernel(tc, h2, W3, b3, W4, b4, out):
         nc.gpsimd.memset(b4_padded[:].bitcast(F32), 0.0)
         identity = const.tile([P, P], F32)
         make_identity(nc, identity[:])
+        identity_bf16 = const.tile([P, P], BF16)
+        make_identity(nc, identity_bf16[:])
         ones = const.tile([P, P], BF16)
         nc.vector.memset(ones[:], 1.0)
         table_in = const.tile([P, 1], F32)
@@ -256,11 +281,11 @@ def tile_environvectorfield_pb_kernel(tc, h2, W3, b3, W4, b4, out):
         b3_cols = const.tile([P, E * H // P], F32)
         nc.vector.tensor_copy(out=b3_cols[:], in_=b3_bank[:, 0 : E * H // P])
         b4_all = const.tile([P, E * D], F32)
-        for c in range(E * D // (2 * D)):
-            cols = slice(2 * D * c, 2 * D * (c + 1))
-            b4_bank = ps_second.tile([P, 2 * D], F32, name="b4_bank", tag="small_bank")
+        for c in range(E * D // (2 * B)):
+            cols = slice(2 * B * c, 2 * B * (c + 1))
+            b4_bank = ps_first.tile([P, 2 * B], F32, name="b4_bank", tag="h3_bank")
             nc.tensor.matmul(b4_bank[:], lhsT=ones[:], rhs=b4_padded[:, cols], start=True, stop=True)
-            nc.scalar.copy(out=b4_all[:, cols], in_=b4_bank[:])
+            nc.vector.tensor_copy(out=b4_all[:, cols], in_=b4_bank[:])
 
         out_tile = const.tile([P, 2 * E * D], F32)
         out_rows = out_tile[:].rearrange("p (i x) -> p i x", i=2)
@@ -269,10 +294,14 @@ def tile_environvectorfield_pb_kernel(tc, h2, W3, b3, W4, b4, out):
             e, h = s // 2, s % 2
             if h == 0 and e < E:
                 transpose_h2(e)
+            if s in MOVED:
+                move_w3(s)
             if 0 <= s - 1 < HALVES:
                 quantise_w3(s - 1)
             if s < HALVES:
                 regroup_w3(s, 0)
+            if s in MOVED:
+                copy_moved(s)
             if 0 <= s - 3 < HALVES:
                 regroup_h3(s - 3)
             if s < HALVES:

@@ -294,8 +294,6 @@ def tile_environvectorfield_pb_kernel(tc, h2, W3, b3, W4, b4, out):
             e, h = s // 2, s % 2
             if h == 0 and e < E:
                 transpose_h2(e)
-            if s in MOVED:
-                move_w3(s)
             if 0 <= s - 1 < HALVES:
                 quantise_w3(s - 1)
             if s < HALVES:
@@ -310,6 +308,8 @@ def tile_environvectorfield_pb_kernel(tc, h2, W3, b3, W4, b4, out):
                 quantise_h2(e)
             if 0 <= s - 1 < HALVES:
                 first_product(s - 1)
+            if s + 1 in MOVED:
+                move_w3(s + 1)
             if 0 <= s - 2 < HALVES:
                 swish(s - 2)
             if h == 0 and e < E:

@@ -48,10 +48,9 @@ def tile_environvectorfield_pb_kernel(tc, h2, W3, b3, W4, b4, out):
         w4_in = ctx.enter_context(tc.tile_pool(name="w4_in", bufs=E))
         three = ctx.enter_context(tc.tile_pool(name="three", bufs=3))
         two = ctx.enter_context(tc.tile_pool(name="two", bufs=2))
-        ps_h2 = ctx.enter_context(tc.psum_pool(name="ps_h2", bufs=2))
+        ps_turn = ctx.enter_context(tc.psum_pool(name="ps_turn", bufs=3))
         ps_first = ctx.enter_context(tc.psum_pool(name="ps_first", bufs=4))
         ps_second = ctx.enter_context(tc.psum_pool(name="ps_second", bufs=1))
-        ps_move = ctx.enter_context(tc.psum_pool(name="ps_move", bufs=1))
         ctx.enter_context(tc.manual_schedule())
 
         live = {}
@@ -88,7 +87,7 @@ def tile_environvectorfield_pb_kernel(tc, h2, W3, b3, W4, b4, out):
         def transpose_h2(e):
             words = live[("h2_raw", e)][:].bitcast(F32)
             for g in range(2):
-                bank = ps_h2.tile([P, 2 * B], F32, name="h2_bank", tag="h2_bank")
+                bank = ps_turn.tile([P, 2 * B], F32, name="h2_bank", tag="turn_bank")
                 for u in range(2):
                     for i in range(2):
                         first = i * (H // 2) + g * (HALF // 2)
@@ -116,7 +115,7 @@ def tile_environvectorfield_pb_kernel(tc, h2, W3, b3, W4, b4, out):
             live[("h2_mx", e)] = (codes, scales)
 
         def move_w3(s):
-            bank = ps_move.tile([P, PACK * QUARTER], BF16, name="w3_bank", tag="w3_bank")
+            bank = ps_turn.tile([P, PACK * QUARTER], BF16, name="w3_bank", tag="turn_bank")
             by_word = live[("w3_raw", s, s % 2)].rearrange("p t n -> p n t")
             for c in range(0, QUARTER, P):
                 nc.tensor.matmul(
@@ -306,9 +305,11 @@ def tile_environvectorfield_pb_kernel(tc, h2, W3, b3, W4, b4, out):
                 regroup_w3(s, 1)
             if h == 1 and e < E:
                 quantise_h2(e)
+            if h == 1 and s + 1 in MOVED:
+                move_w3(s + 1)
             if 0 <= s - 1 < HALVES:
                 first_product(s - 1)
-            if s + 1 in MOVED:
+            if h == 0 and s + 1 in MOVED:
                 move_w3(s + 1)
             if 0 <= s - 2 < HALVES:
                 swish(s - 2)

@@ -17,10 +17,11 @@ B, E, D, H = 256, 8, 128, 1024
 HALVES = 2 * E
 HALF = H // 2
 QUARTER = HALF // 2
+B3_ROWS = E * H // P
 FLOPS = 2 * E * B * H * (H + D)
 
 W3_LOAD_AFTER_STEP = {0: 3, 1: 4, 3: 5, 5: 6, 7: 7}
-MOVED = range(2, HALVES - 2)
+MOVED = range(2, HALVES)
 STORE_AFTER = {3: 0, 5: 4, 6: 6, 7: 7}
 
 
@@ -38,7 +39,6 @@ def tile_environvectorfield_pb_kernel(tc, h2, W3, b3, W4, b4, out):
     w3_planes = W3.rearrange("e (g p t) n -> e g p t n", g=2, p=P, t=PACK)
     w4_view = W4.rearrange("e (a p) d -> e p a d", p=P)
     b3_rows = b3.rearrange("e (j q) -> (e j) q", q=P)
-    b4_row = b4.rearrange("(o e) d -> o (e d)", o=1)
     out_view = out.rearrange("(p i e) d -> p i (e d)", i=2, e=E)
 
     with ExitStack() as ctx:
@@ -130,7 +130,8 @@ def tile_environvectorfield_pb_kernel(tc, h2, W3, b3, W4, b4, out):
         def copy_moved(s):
             first = PACK * (HALF * (s % 2) + QUARTER)
             nc.scalar.copy(
-                out=live[("w3_grouped", s)][:, first : first + PACK * QUARTER], in_=live[("w3_bank", s)][:]
+                out=live[("w3_grouped", s)][:, first : first + PACK * QUARTER].bitcast(F32),
+                in_=live[("w3_bank", s)][:].bitcast(F32),
             )
 
         def regroup_w3(s, g):
@@ -179,7 +180,7 @@ def tile_environvectorfield_pb_kernel(tc, h2, W3, b3, W4, b4, out):
                     out=h3_planes[:, B * t : B * (t + 1)],
                     in_=live[("h3_bank", s, t // 2)][:, B * (t % 2) : B * (t % 2 + 1)],
                     func=ACT.Silu,
-                    bias=b3_cols[:, PACK * s + t : PACK * s + t + 1],
+                    bias=bias_cols[:, PACK * s + t : PACK * s + t + 1],
                     scale=1.0,
                 )
             live[("h3_planes", s)] = h3_planes
@@ -248,24 +249,44 @@ def tile_environvectorfield_pb_kernel(tc, h2, W3, b3, W4, b4, out):
             cols = slice(D * first, D * (last + 1))
             nc.sync.dma_start(out=out_view[:, :, cols], in_=out_rows[:, :, cols])
 
-        b3_padded = const.tile([P, P], BF16)
-        nc.gpsimd.memset(b3_padded[:].bitcast(F32), 0.0)
-        b4_padded = const.tile([P, E * D], BF16)
-        nc.gpsimd.memset(b4_padded[:].bitcast(F32), 0.0)
+        def turn_biases():
+            nc.vector.tensor_copy(out=biases_f32[:], in_=biases[:])
+            bias_bank = ps_second.tile([P, 2 * D], F32, name="bias_bank", tag="small_bank")
+            nc.tensor.transpose(bias_bank[:, 0:P], biases_f32[:], identity[:])
+            nc.vector.tensor_copy(out=bias_cols[:], in_=bias_bank[:, 0:P])
+
+        def spread_b4():
+            for c in range(2):
+                b4_bank = ps_first.tile([P, PACK * D], F32, name="b4_bank", tag="h3_bank")
+                for i in range(PACK):
+                    col = B3_ROWS + PACK * c + i
+                    nc.tensor.transpose(
+                        b4_bank[:, D * i : D * (i + 1)],
+                        bias_cols[:, col : col + 1].to_broadcast([P, P]),
+                        identity[:],
+                    )
+                live[("b4_bank", c)] = b4_bank
+
+        def copy_b4():
+            for c in range(2):
+                nc.vector.tensor_copy(
+                    out=b4_all[:, PACK * D * c : PACK * D * (c + 1)], in_=live[("b4_bank", c)][:]
+                )
+
+        biases = const.tile([P, P], BF16)
+        nc.gpsimd.memset(biases[:].bitcast(F32), 0.0)
         identity = const.tile([P, P], F32)
         make_identity(nc, identity[:])
         identity_bf16 = const.tile([P, P], BF16)
         make_identity(nc, identity_bf16[:])
-        ones = const.tile([P, P], BF16)
-        nc.vector.memset(ones[:], 1.0)
         table_in = const.tile([P, 1], F32)
         nc.vector.memset(table_in[:], 0.0)
         table_out = const.tile([P, 1], F32)
         nc.scalar.activation(out=table_out[:], in_=table_in[:], func=ACT.Silu)
 
-        nc.sync.dma_start(out=b3_padded[0 : E * H // P, :], in_=b3_rows)
-        nc.sync.dma_start(out=b4_padded[0:1, :], in_=b4_row)
         load_w3_piece(0, 0)
+        nc.sync.dma_start(out=biases[0:B3_ROWS, :], in_=b3_rows)
+        nc.sync.dma_start(out=biases[B3_ROWS : B3_ROWS + E, :], in_=b4)
         load_w3_piece(1, 0)
         load_h2(0)
         load_w3_piece(0, 1)
@@ -273,19 +294,9 @@ def tile_environvectorfield_pb_kernel(tc, h2, W3, b3, W4, b4, out):
         load_environment(1)
         load_environment(2)
 
-        b3_f32 = const.tile([P, P], F32)
-        nc.vector.tensor_copy(out=b3_f32[:], in_=b3_padded[:])
-        b3_bank = ps_second.tile([P, 2 * D], F32, name="b3_bank", tag="small_bank")
-        nc.tensor.transpose(b3_bank[:, 0:P], b3_f32[:], identity[:])
-        b3_cols = const.tile([P, E * H // P], F32)
-        nc.vector.tensor_copy(out=b3_cols[:], in_=b3_bank[:, 0 : E * H // P])
+        biases_f32 = const.tile([P, P], F32)
+        bias_cols = const.tile([P, P], F32)
         b4_all = const.tile([P, E * D], F32)
-        for c in range(E * D // (2 * B)):
-            cols = slice(2 * B * c, 2 * B * (c + 1))
-            b4_bank = ps_first.tile([P, 2 * B], F32, name="b4_bank", tag="h3_bank")
-            nc.tensor.matmul(b4_bank[:], lhsT=ones[:], rhs=b4_padded[:, cols], start=True, stop=True)
-            nc.vector.tensor_copy(out=b4_all[:, cols], in_=b4_bank[:])
-
         out_tile = const.tile([P, 2 * E * D], F32)
         out_rows = out_tile[:].rearrange("p (i x) -> p i x", i=2)
 
@@ -295,6 +306,9 @@ def tile_environvectorfield_pb_kernel(tc, h2, W3, b3, W4, b4, out):
                 transpose_h2(e)
             if 0 <= s - 1 < HALVES:
                 quantise_w3(s - 1)
+            if s == 1:
+                turn_biases()
+                spread_b4()
             if s < HALVES:
                 regroup_w3(s, 0)
             if s in MOVED:
@@ -309,6 +323,8 @@ def tile_environvectorfield_pb_kernel(tc, h2, W3, b3, W4, b4, out):
                 move_w3(s + 1)
             if 0 <= s - 1 < HALVES:
                 first_product(s - 1)
+            if s == 1:
+                copy_b4()
             if h == 0 and s + 1 in MOVED:
                 move_w3(s + 1)
             if 0 <= s - 2 < HALVES:

@@ -116,15 +116,12 @@ def tile_environvectorfield_pb_kernel(tc, h2, W3, b3, W4, b4, out):
 
         def move_w3(s):
             bank = ps_turn.tile([P, PACK * QUARTER], BF16, name="w3_bank", tag="turn_bank")
-            by_word = live[("w3_raw", s, s % 2)].rearrange("p t n -> p n t")
             for c in range(0, QUARTER, P):
-                nc.tensor.matmul(
+                grouped, planes = regroup_views(
                     bank[:, PACK * c : PACK * (c + P)],
-                    lhsT=identity_bf16[:],
-                    rhs=by_word[:, QUARTER + c : QUARTER + c + P, :],
-                    start=True,
-                    stop=True,
+                    live[("w3_raw", s, s % 2)][:, :, QUARTER + c : QUARTER + c + P],
                 )
+                nc.tensor.matmul(grouped, lhsT=identity_bf16[:], rhs=planes, start=True, stop=True)
             live[("w3_bank", s)] = bank
 
         def copy_moved(s):

@@ -20,9 +20,14 @@ QUARTER = HALF // 2
 B3_ROWS = E * H // P
 FLOPS = 2 * E * B * H * (H + D)
 
-W3_LOAD_AFTER_STEP = {0: 3, 1: 4, 3: 5, 5: 6, 7: 7}
+W3_LOAD_AFTER_STEP = {1: 4, 3: 5, 5: 6, 7: 7}
+EARLY = 1
 MOVED = range(2, HALVES)
 STORE_AFTER = {3: 0, 5: 4, 6: 6, 7: 7}
+
+
+def moved_pass(s):
+    return 1 if s >= HALVES - 2 else s % 2
 
 
 def regroup_views(grouped, planes):
@@ -36,7 +41,6 @@ def tile_environvectorfield_pb_kernel(tc, h2, W3, b3, W4, b4, out):
     nc = tc.nc
     h2_view = h2.rearrange("(p i) e k -> e p i k", i=2)
     w3_tiles = W3.rearrange("e (g p t) n -> e g p (t n)", g=2, p=P, t=PACK)
-    w3_planes = W3.rearrange("e (g p t) n -> e g p t n", g=2, p=P, t=PACK)
     w4_view = W4.rearrange("e (a p) d -> e p a d", p=P)
     b3_rows = b3.rearrange("e (j q) -> (e j) q", q=P)
     out_view = out.rearrange("(p i e) d -> p i (e d)", i=2, e=E)
@@ -54,12 +58,6 @@ def tile_environvectorfield_pb_kernel(tc, h2, W3, b3, W4, b4, out):
         ctx.enter_context(tc.manual_schedule())
 
         live = {}
-
-        def load_w3_piece(g, h):
-            w3_raw = w3_in.tile([P, PACK * HALF], BF16, name="w3_raw", tag="w3_raw")
-            planes = w3_raw[:].rearrange("p (t n) -> p t n", t=PACK)
-            nc.sync.dma_start(out=planes, in_=w3_planes[0, g][:, :, HALF * h : HALF * (h + 1)])
-            live[("w3_raw", h, g)] = planes
 
         def load_w3(e, g):
             w3_raw = w3_in.tile([P, PACK * H], BF16, name="w3_raw", tag="w3_raw")
@@ -82,7 +80,8 @@ def tile_environvectorfield_pb_kernel(tc, h2, W3, b3, W4, b4, out):
             load_w3(e, 0)
             load_w3(e, 1)
             load_h2(e)
-            load_w4(e - 1)
+            for w4_of in {1: (), 2: (0, 1)}.get(e, (e - 1,)):
+                load_w4(w4_of)
 
         def transpose_h2(e):
             words = live[("h2_raw", e)][:].bitcast(F32)
@@ -119,29 +118,26 @@ def tile_environvectorfield_pb_kernel(tc, h2, W3, b3, W4, b4, out):
             for c in range(0, QUARTER, P):
                 grouped, planes = regroup_views(
                     bank[:, PACK * c : PACK * (c + P)],
-                    live[("w3_raw", s, s % 2)][:, :, QUARTER + c : QUARTER + c + P],
+                    live[("w3_raw", s, moved_pass(s))][:, :, QUARTER + c : QUARTER + c + P],
                 )
                 nc.tensor.matmul(grouped, lhsT=identity_bf16[:], rhs=planes, start=True, stop=True)
             live[("w3_bank", s)] = bank
 
         def copy_moved(s):
-            first = PACK * (HALF * (s % 2) + QUARTER)
+            first = PACK * (HALF * moved_pass(s) + QUARTER)
             nc.scalar.copy(
                 out=live[("w3_grouped", s)][:, first : first + PACK * QUARTER].bitcast(F32),
                 in_=live[("w3_bank", s)][:].bitcast(F32),
             )
 
-        def regroup_w3(s, g):
-            if g == 0:
+        def regroup_w3(copy, s, g):
+            if ("w3_grouped", s) not in live:
                 w3_new = three.tile([P, 2 * PACK * HALF], BF16, name="w3_grouped", tag="w3_grouped", align_bytes=64)
                 live[("w3_grouped", s)] = w3_new
-            n = QUARTER if s in MOVED and g == s % 2 else HALF
+            n = QUARTER if s in MOVED and g == moved_pass(s) else HALF
             chunk = live[("w3_grouped", s)][:, PACK * HALF * g : PACK * (HALF * g + n)]
             grouped, planes = regroup_views(chunk, live[("w3_raw", s, g)][:, :, 0:n])
-            if g == 0:
-                nc.scalar.copy(out=grouped, in_=planes)
-            else:
-                nc.vector.tensor_copy(out=grouped, in_=planes)
+            copy(out=grouped, in_=planes)
 
         def quantise_w3(s):
             codes = three.tile([P, 2 * HALF], U32, name="w3_codes", tag="w3_codes", align_bytes=64)
@@ -281,15 +277,14 @@ def tile_environvectorfield_pb_kernel(tc, h2, W3, b3, W4, b4, out):
         table_out = const.tile([P, 1], F32)
         nc.scalar.activation(out=table_out[:], in_=table_in[:], func=ACT.Silu)
 
-        load_w3_piece(0, 0)
+        load_w3(0, 0)
         nc.sync.dma_start(out=biases[0:B3_ROWS, :], in_=b3_rows)
         nc.sync.dma_start(out=biases[B3_ROWS : B3_ROWS + E, :], in_=b4)
-        load_w3_piece(1, 0)
+        load_w3(0, 1)
         load_h2(0)
-        load_w3_piece(0, 1)
-        load_w3_piece(1, 1)
         load_environment(1)
         load_environment(2)
+        load_environment(3)
 
         biases_f32 = const.tile([P, P], F32)
         bias_cols = const.tile([P, P], F32)
@@ -299,34 +294,43 @@ def tile_environvectorfield_pb_kernel(tc, h2, W3, b3, W4, b4, out):
 
         for s in range(HALVES + 4):
             e, h = s // 2, s % 2
-            if h == 0 and e < E:
+            early = e < EARLY
+            h2_now = e < E and h == (1 if early else 0)
+            if h2_now and not early:
                 transpose_h2(e)
             if 0 <= s - 1 < HALVES:
                 quantise_w3(s - 1)
-            if s == 1:
-                turn_biases()
-                spread_b4()
+            if s == 2:
+                copy_b4()
+            if s == 4:
+                regroup_w4(0)
             if s < HALVES:
-                regroup_w3(s, 0)
+                regroup_w3(nc.scalar.copy, s, 1 if early and h == 1 else 0)
             if s in MOVED:
                 copy_moved(s)
             if 0 <= s - 3 < HALVES:
                 regroup_h3(s - 3)
-            if s < HALVES:
-                regroup_w3(s, 1)
-            if h == 1 and e < E:
-                quantise_h2(e)
+            if early and h == 0:
+                regroup_w3(nc.vector.tensor_copy, s + 1, 0)
+            if s == 0:
+                turn_biases()
+                spread_b4()
+            if s < HALVES and not (early and h == 1):
+                regroup_w3(nc.vector.tensor_copy, s, 1)
+            if h2_now and early:
+                transpose_h2(e)
+                copy_h2(e)
             if h == 1 and s + 1 in MOVED:
                 move_w3(s + 1)
+            if h == 1 and e < E:
+                quantise_h2(e)
             if 0 <= s - 1 < HALVES:
                 first_product(s - 1)
-            if s == 1:
-                copy_b4()
             if h == 0 and s + 1 in MOVED:
                 move_w3(s + 1)
             if 0 <= s - 2 < HALVES:
                 swish(s - 2)
-            if h == 0 and e < E:
+            if h2_now and not early:
                 copy_h2(e)
             if h == 0 and 0 <= e - 2 < E:
                 quantise_w4(e - 2)
@@ -334,7 +338,7 @@ def tile_environvectorfield_pb_kernel(tc, h2, W3, b3, W4, b4, out):
                 quantise_h3(s - 3)
                 if h == 0:
                     second_product(e - 2)
-            if h == 1 and 0 <= e - 1 < E:
+            if h == 1 and 1 <= e - 1 < E:
                 regroup_w4(e - 1)
             if h == 1 and 0 <= e - 2 < E:
                 add_b4(e - 2)

@@ -27,7 +27,7 @@ STORE_AFTER = {3: 0, 5: 4, 6: 6, 7: 7}
 
 
 def moved_pass(s):
-    return 1 if s >= HALVES - 2 else s % 2
+    return 1 if s % 4 == 1 or s == HALVES - 1 else 0
 
 
 def regroup_views(grouped, planes):
@@ -246,26 +246,9 @@ def tile_environvectorfield_pb_kernel(tc, h2, W3, b3, W4, b4, out):
             nc.vector.tensor_copy(out=biases_f32[:], in_=biases[:])
             bias_bank = ps_second.tile([P, 2 * D], F32, name="bias_bank", tag="small_bank")
             nc.tensor.transpose(bias_bank[:, 0:P], biases_f32[:], identity[:])
-            nc.vector.tensor_copy(out=bias_cols[:], in_=bias_bank[:, 0:P])
+            live["bias_bank"] = bias_bank
 
-        def spread_b4():
-            for c in range(2):
-                b4_bank = ps_first.tile([P, PACK * D], F32, name="b4_bank", tag="h3_bank")
-                for i in range(PACK):
-                    col = B3_ROWS + PACK * c + i
-                    nc.tensor.transpose(
-                        b4_bank[:, D * i : D * (i + 1)],
-                        bias_cols[:, col : col + 1].to_broadcast([P, P]),
-                        identity[:],
-                    )
-                live[("b4_bank", c)] = b4_bank
-
-        def copy_b4():
-            for c in range(2):
-                nc.vector.tensor_copy(
-                    out=b4_all[:, PACK * D * c : PACK * D * (c + 1)], in_=live[("b4_bank", c)][:]
-                )
-
+        b4_all = const.tile([P, E * D], BF16)
         biases = const.tile([P, P], BF16)
         nc.gpsimd.memset(biases[:].bitcast(F32), 0.0)
         identity = const.tile([P, P], F32)
@@ -277,31 +260,30 @@ def tile_environvectorfield_pb_kernel(tc, h2, W3, b3, W4, b4, out):
         table_out = const.tile([P, 1], F32)
         nc.scalar.activation(out=table_out[:], in_=table_in[:], func=ACT.Silu)
 
+        load_h2(0)
         load_w3(0, 0)
         nc.sync.dma_start(out=biases[0:B3_ROWS, :], in_=b3_rows)
-        nc.sync.dma_start(out=biases[B3_ROWS : B3_ROWS + E, :], in_=b4)
         load_w3(0, 1)
-        load_h2(0)
         load_environment(1)
         load_environment(2)
+        nc.sync.dma_start(out=b4_all[:], in_=b4.rearrange("e d -> (e d)").partition_broadcast(P))
         load_environment(3)
 
         biases_f32 = const.tile([P, P], F32)
         bias_cols = const.tile([P, P], F32)
-        b4_all = const.tile([P, E * D], F32)
         out_tile = const.tile([P, 2 * E * D], F32)
         out_rows = out_tile[:].rearrange("p (i x) -> p i x", i=2)
 
         for s in range(HALVES + 4):
             e, h = s // 2, s % 2
             early = e < EARLY
-            h2_now = e < E and h == (1 if early else 0)
-            if h2_now and not early:
+            if h == 0 and e < E:
                 transpose_h2(e)
+            if s == 0:
+                copy_h2(0)
+                quantise_h2(0)
             if 0 <= s - 1 < HALVES:
                 quantise_w3(s - 1)
-            if s == 2:
-                copy_b4()
             if s == 4:
                 regroup_w4(0)
             if s < HALVES:
@@ -314,15 +296,13 @@ def tile_environvectorfield_pb_kernel(tc, h2, W3, b3, W4, b4, out):
                 regroup_w3(nc.vector.tensor_copy, s + 1, 0)
             if s == 0:
                 turn_biases()
-                spread_b4()
             if s < HALVES and not (early and h == 1):
                 regroup_w3(nc.vector.tensor_copy, s, 1)
-            if h2_now and early:
-                transpose_h2(e)
-                copy_h2(e)
+            if s == 0:
+                nc.vector.tensor_copy(out=bias_cols[:], in_=live["bias_bank"][:, 0:P])
             if h == 1 and s + 1 in MOVED:
                 move_w3(s + 1)
-            if h == 1 and e < E:
+            if h == 1 and 0 < e < E:
                 quantise_h2(e)
             if 0 <= s - 1 < HALVES:
                 first_product(s - 1)
@@ -330,7 +310,7 @@ def tile_environvectorfield_pb_kernel(tc, h2, W3, b3, W4, b4, out):
                 move_w3(s + 1)
             if 0 <= s - 2 < HALVES:
                 swish(s - 2)
-            if h2_now and not early:
+            if h == 0 and 0 < e < E:
                 copy_h2(e)
             if h == 0 and 0 <= e - 2 < E:
                 quantise_w4(e - 2)

@@ -183,7 +183,10 @@ def tile_environvectorfield_pb_kernel(tc, h2, W3, b3, W4, b4, out):
             grouped, planes = regroup_views(
                 h3_grouped[:], live[("h3_planes", s)][:].rearrange("p (t b) -> p t b", t=PACK)
             )
-            nc.vector.tensor_copy(out=grouped, in_=planes)
+            if s == HALVES - 3:
+                nc.scalar.copy(out=grouped, in_=planes)
+            else:
+                nc.vector.tensor_copy(out=grouped, in_=planes)
             live[("h3_grouped", s)] = h3_grouped
 
         def quantise_h3(s):
@@ -199,10 +202,12 @@ def tile_environvectorfield_pb_kernel(tc, h2, W3, b3, W4, b4, out):
 
         def regroup_w4(e):
             w4_grouped = three.tile([P, 2 * PACK * D], BF16, name="w4_grouped", tag="w4_grouped", align_bytes=64)
-            nc.vector.tensor_copy(
-                out=w4_grouped[:].rearrange("p (h c i t) -> p h c t i", h=2, i=4, t=PACK),
-                in_=live[("w4_raw", e)][:].rearrange("p (h t c i) -> p h c t i", h=2, t=PACK, i=4),
-            )
+            grouped = w4_grouped[:].rearrange("p (h c i t) -> p h c t i", h=2, i=4, t=PACK)
+            planes = live[("w4_raw", e)][:].rearrange("p (h t c i) -> p h c t i", h=2, t=PACK, i=4)
+            if e == E - 1:
+                nc.scalar.copy(out=grouped, in_=planes)
+            else:
+                nc.vector.tensor_copy(out=grouped, in_=planes)
             live[("w4_grouped", e)] = w4_grouped
 
         def quantise_w4(e):
@@ -248,7 +253,22 @@ def tile_environvectorfield_pb_kernel(tc, h2, W3, b3, W4, b4, out):
             nc.tensor.transpose(bias_bank[:, 0:P], biases_f32[:], identity[:])
             live["bias_bank"] = bias_bank
 
-        b4_all = const.tile([P, E * D], BF16)
+        def spread_b4():
+            for c in range(2):
+                b4_bank = ps_first.tile([P, PACK * D], F32, name="b4_bank", tag="h3_bank")
+                for i in range(PACK):
+                    col = B3_ROWS + PACK * c + i
+                    nc.tensor.transpose(
+                        b4_bank[:, D * i : D * (i + 1)],
+                        bias_cols[:, col : col + 1].to_broadcast([P, P]),
+                        identity[:],
+                    )
+                live[("b4_bank", c)] = b4_bank
+
+        def copy_b4():
+            for c in range(2):
+                nc.scalar.copy(out=b4_all[:, PACK * D * c : PACK * D * (c + 1)], in_=live[("b4_bank", c)][:])
+
         biases = const.tile([P, P], BF16)
         nc.gpsimd.memset(biases[:].bitcast(F32), 0.0)
         identity = const.tile([P, P], F32)
@@ -263,14 +283,15 @@ def tile_environvectorfield_pb_kernel(tc, h2, W3, b3, W4, b4, out):
         load_h2(0)
         load_w3(0, 0)
         nc.sync.dma_start(out=biases[0:B3_ROWS, :], in_=b3_rows)
+        nc.sync.dma_start(out=biases[B3_ROWS : B3_ROWS + E, :], in_=b4)
         load_w3(0, 1)
         load_environment(1)
         load_environment(2)
-        nc.sync.dma_start(out=b4_all[:], in_=b4.rearrange("e d -> (e d)").partition_broadcast(P))
         load_environment(3)
 
         biases_f32 = const.tile([P, P], F32)
         bias_cols = const.tile([P, P], F32)
+        b4_all = const.tile([P, E * D], F32)
         out_tile = const.tile([P, 2 * E * D], F32)
         out_rows = out_tile[:].rearrange("p (i x) -> p i x", i=2)
 
@@ -284,14 +305,16 @@ def tile_environvectorfield_pb_kernel(tc, h2, W3, b3, W4, b4, out):
                 quantise_h2(0)
             if 0 <= s - 1 < HALVES:
                 quantise_w3(s - 1)
-            if s == 4:
-                regroup_w4(0)
             if s < HALVES:
                 regroup_w3(nc.scalar.copy, s, 1 if early and h == 1 else 0)
+            if s == 1:
+                copy_b4()
             if s in MOVED:
                 copy_moved(s)
             if 0 <= s - 3 < HALVES:
                 regroup_h3(s - 3)
+            if s == 4:
+                regroup_w4(0)
             if early and h == 0:
                 regroup_w3(nc.vector.tensor_copy, s + 1, 0)
             if s == 0:
@@ -300,6 +323,7 @@ def tile_environvectorfield_pb_kernel(tc, h2, W3, b3, W4, b4, out):
                 regroup_w3(nc.vector.tensor_copy, s, 1)
             if s == 0:
                 nc.vector.tensor_copy(out=bias_cols[:], in_=live["bias_bank"][:, 0:P])
+                spread_b4()
             if h == 1 and s + 1 in MOVED:
                 move_w3(s + 1)
             if h == 1 and 0 < e < E:
@@ -318,8 +342,10 @@ def tile_environvectorfield_pb_kernel(tc, h2, W3, b3, W4, b4, out):
                 quantise_h3(s - 3)
                 if h == 0:
                     second_product(e - 2)
-            if h == 1 and 1 <= e - 1 < E:
+            if h == 1 and 1 <= e - 1 < E - 1:
                 regroup_w4(e - 1)
+            if s == HALVES - 1:
+                regroup_w4(E - 1)
             if h == 1 and 0 <= e - 2 < E:
                 add_b4(e - 2)
                 if e - 2 in STORE_AFTER:

from contextlib import ExitStack

import concourse.mybir as mybir
from concourse.masks import make_identity

BF16 = mybir.dt.bfloat16
F32 = mybir.dt.float32
U32 = mybir.dt.uint32
U8 = mybir.dt.uint8
FP8X4 = mybir.dt.float8_e4m3fn_x4
ACT = mybir.ActivationFunctionType
ALU = mybir.AluOpType

P = 128
PACK = 4
B, E, D, H = 256, 8, 128, 1024
HALVES = 2 * E
HALF = H // 2
QUARTER = HALF // 2
B3_ROWS = E * H // P
FLOPS = 2 * E * B * H * (H + D)

W3_LOAD_AFTER_STEP = {1: 4, 3: 5, 5: 6, 7: 7}
EARLY = 1
MOVED = range(2, HALVES)
STORE_AFTER = {3: 0, 5: 4, 6: 6, 7: 7}


def moved_pass(s):
    return 1 if s % 4 == 1 or s == HALVES - 1 else 0


def regroup_views(grouped, planes):
    return (
        grouped.rearrange("p (c i t) -> p c t i", i=4, t=PACK),
        planes.rearrange("p t (c i) -> p c t i", i=4),
    )


def tile_environvectorfield_pb_kernel(tc, h2, W3, b3, W4, b4, out):
    nc = tc.nc
    h2_view = h2.rearrange("(p i) e k -> e p i k", i=2)
    w3_tiles = W3.rearrange("e (g p t) n -> e g p (t n)", g=2, p=P, t=PACK)
    w4_view = W4.rearrange("e (a p) d -> e p a d", p=P)
    b3_rows = b3.rearrange("e (j q) -> (e j) q", q=P)
    out_view = out.rearrange("(p i e) d -> p i (e d)", i=2, e=E)

    with ExitStack() as ctx:
        const = ctx.enter_context(tc.tile_pool(name="const", bufs=1))
        w3_in = ctx.enter_context(tc.tile_pool(name="w3_in", bufs=8))
        h2_in = ctx.enter_context(tc.tile_pool(name="h2_in", bufs=E))
        w4_in = ctx.enter_context(tc.tile_pool(name="w4_in", bufs=E))
        three = ctx.enter_context(tc.tile_pool(name="three", bufs=3))
        two = ctx.enter_context(tc.tile_pool(name="two", bufs=2))
        ps_turn = ctx.enter_context(tc.psum_pool(name="ps_turn", bufs=3))
        ps_first = ctx.enter_context(tc.psum_pool(name="ps_first", bufs=4))
        ps_second = ctx.enter_context(tc.psum_pool(name="ps_second", bufs=1))
        ctx.enter_context(tc.manual_schedule())

        live = {}

        def load_w3(e, g):
            w3_raw = w3_in.tile([P, PACK * H], BF16, name="w3_raw", tag="w3_raw")
            nc.sync.dma_start(out=w3_raw[:], in_=w3_tiles[e, g])
            planes = w3_raw[:].rearrange("p (t n) -> p t n", t=PACK)
            for h in range(2):
                live[("w3_raw", 2 * e + h, g)] = planes[:, :, HALF * h : HALF * (h + 1)]

        def load_h2(e):
            h2_raw = h2_in.tile([P, 2 * H], BF16, name="h2_raw", tag="h2_raw")
            nc.sync.dma_start(out=h2_raw[:].rearrange("p (i k) -> p i k", i=2), in_=h2_view[e])
            live[("h2_raw", e)] = h2_raw

        def load_w4(e):
            w4_raw = w4_in.tile([P, 2 * PACK * D], BF16, name="w4_raw", tag="w4_raw")
            nc.sync.dma_start(out=w4_raw[:].rearrange("p (a d) -> p a d", a=2 * PACK), in_=w4_view[e])
            live[("w4_raw", e)] = w4_raw

        def load_environment(e):
            load_w3(e, 0)
            load_w3(e, 1)
            load_h2(e)
            for w4_of in {1: (), 2: (0, 1)}.get(e, (e - 1,)):
                load_w4(w4_of)

        def transpose_h2(e):
            words = live[("h2_raw", e)][:].bitcast(F32)
            for g in range(2):
                bank = ps_turn.tile([P, 2 * B], F32, name="h2_bank", tag="turn_bank")
                for u in range(2):
                    for i in range(2):
                        first = i * (H // 2) + g * (HALF // 2)
                        nc.tensor.transpose(
                            bank[:, u * B + i * P : u * B + (i + 1) * P],
                            words[:, first : first + HALF // 2].rearrange("p (w u) -> p u w", u=2)[:, u, :],
                            identity[:],
                        )
                live[("h2_bank", e, g)] = bank

        def copy_h2(e):
            h2_grouped = two.tile([P, 2 * PACK * B], BF16, name="h2_grouped", tag="h2_grouped", align_bytes=64)
            words = h2_grouped[:].bitcast(F32)
            for g in range(2):
                nc.scalar.copy(
                    out=words[:, 2 * B * g : 2 * B * (g + 1)].rearrange("p (b u) -> p b u", u=2),
                    in_=live[("h2_bank", e, g)][:].rearrange("p (u b) -> p b u", u=2),
                )
            live[("h2_grouped", e)] = h2_grouped

        def quantise_h2(e):
            codes = two.tile([P, 2 * B], U32, name="h2_codes", tag="h2_codes", align_bytes=64)
            scales = two.tile([P, 2 * B], U8, name="h2_scales", tag="h2_scales", align_bytes=64)
            nc.vector.quantize_mx(out=codes[:].bitcast(FP8X4), scales=scales[:], in_=live[("h2_grouped", e)][:])
            live[("h2_mx", e)] = (codes, scales)

        def move_w3(s):
            bank = ps_turn.tile([P, PACK * QUARTER], BF16, name="w3_bank", tag="turn_bank")
            for c in range(0, QUARTER, P):
                grouped, planes = regroup_views(
                    bank[:, PACK * c : PACK * (c + P)],
                    live[("w3_raw", s, moved_pass(s))][:, :, QUARTER + c : QUARTER + c + P],
                )
                nc.tensor.matmul(grouped, lhsT=identity_bf16[:], rhs=planes, start=True, stop=True)
            live[("w3_bank", s)] = bank

        def copy_moved(s):
            first = PACK * (HALF * moved_pass(s) + QUARTER)
            nc.scalar.copy(
                out=live[("w3_grouped", s)][:, first : first + PACK * QUARTER].bitcast(F32),
                in_=live[("w3_bank", s)][:].bitcast(F32),
            )

        def regroup_w3(copy, s, g):
            if ("w3_grouped", s) not in live:
                w3_new = three.tile([P, 2 * PACK * HALF], BF16, name="w3_grouped", tag="w3_grouped", align_bytes=64)
                live[("w3_grouped", s)] = w3_new
            n = QUARTER if s in MOVED and g == moved_pass(s) else HALF
            chunk = live[("w3_grouped", s)][:, PACK * HALF * g : PACK * (HALF * g + n)]
            grouped, planes = regroup_views(chunk, live[("w3_raw", s, g)][:, :, 0:n])
            copy(out=grouped, in_=planes)

        def quantise_w3(s):
            codes = three.tile([P, 2 * HALF], U32, name="w3_codes", tag="w3_codes", align_bytes=64)
            scales = three.tile([P, 2 * HALF], U8, name="w3_scales", tag="w3_scales", align_bytes=64)
            nc.vector.quantize_mx(out=codes[:].bitcast(FP8X4), scales=scales[:], in_=live[("w3_grouped", s)][:])
            live[("w3_mx", s)] = (codes, scales)

        def first_product(s):
            w3_codes, w3_scales = live[("w3_mx", s)]
            h2_codes, h2_scales = live[("h2_mx", s // 2)]
            for pair in range(2):
                bank = ps_first.tile([P, 2 * B], F32, name="h3_bank", tag="h3_bank")
                for i in range(2):
                    t = 2 * pair + i
                    for g in range(2):
                        n_cols = slice(HALF * g + P * t, HALF * g + P * (t + 1))
                        b_cols = slice(B * g, B * (g + 1))
                        nc.tensor.matmul_mx(
                            out=bank[:, B * i : B * (i + 1)],
                            lhsT=w3_codes[:, n_cols].bitcast(FP8X4),
                            lhsT_scale=w3_scales[:, n_cols],
                            rhs=h2_codes[:, b_cols].bitcast(FP8X4),
                            rhs_scale=h2_scales[:, b_cols],
                            start=(g == 0),
                            stop=(g == 1),
                        )
                live[("h3_bank", s, pair)] = bank

        def swish(s):
            h3_planes = three.tile([P, PACK * B], BF16, name="h3_planes", tag="h3_planes")
            for t in range(PACK):
                nc.scalar.activation(
                    out=h3_planes[:, B * t : B * (t + 1)],
                    in_=live[("h3_bank", s, t // 2)][:, B * (t % 2) : B * (t % 2 + 1)],
                    func=ACT.Silu,
                    bias=bias_cols[:, PACK * s + t : PACK * s + t + 1],
                    scale=1.0,
                )
            live[("h3_planes", s)] = h3_planes

        def regroup_h3(s):
            h3_grouped = three.tile([P, PACK * B], BF16, name="h3_grouped", tag="h3_grouped", align_bytes=64)
            grouped, planes = regroup_views(
                h3_grouped[:], live[("h3_planes", s)][:].rearrange("p (t b) -> p t b", t=PACK)
            )
            if s == HALVES - 3:
                nc.scalar.copy(out=grouped, in_=planes)
            else:
                nc.vector.tensor_copy(out=grouped, in_=planes)
            live[("h3_grouped", s)] = h3_grouped

        def quantise_h3(s):
            if s % 2 == 0:
                codes_new = two.tile([P, 2 * B], U32, name="h3_codes", tag="h3_codes", align_bytes=64)
                scales_new = two.tile([P, 2 * B], U8, name="h3_scales", tag="h3_scales", align_bytes=64)
                live[("h3_mx", s // 2)] = (codes_new, scales_new)
            codes, scales = live[("h3_mx", s // 2)]
            cols = slice(B * (s % 2), B * (s % 2 + 1))
            nc.vector.quantize_mx(
                out=codes[:, cols].bitcast(FP8X4), scales=scales[:, cols], in_=live[("h3_grouped", s)][:]
            )

        def regroup_w4(e):
            w4_grouped = three.tile([P, 2 * PACK * D], BF16, name="w4_grouped", tag="w4_grouped", align_bytes=64)
            grouped = w4_grouped[:].rearrange("p (h c i t) -> p h c t i", h=2, i=4, t=PACK)
            planes = live[("w4_raw", e)][:].rearrange("p (h t c i) -> p h c t i", h=2, t=PACK, i=4)
            if e == E - 1:
                nc.scalar.copy(out=grouped, in_=planes)
            else:
                nc.vector.tensor_copy(out=grouped, in_=planes)
            live[("w4_grouped", e)] = w4_grouped

        def quantise_w4(e):
            codes = three.tile([P, 2 * D], U32, name="w4_codes", tag="w4_codes", align_bytes=64)
            scales = three.tile([P, 2 * D], U8, name="w4_scales", tag="w4_scales", align_bytes=64)
            nc.vector.quantize_mx(out=codes[:].bitcast(FP8X4), scales=scales[:], in_=live[("w4_grouped", e)][:])
            live[("w4_mx", e)] = (codes, scales)

        def second_product(e):
            h3_codes, h3_scales = live[("h3_mx", e)]
            w4_codes, w4_scales = live[("w4_mx", e)]
            bank = ps_second.tile([P, 2 * D], F32, name="out_bank", tag="small_bank")
            for i in range(2):
                for h in range(2):
                    b_cols = slice(B * h + P * i, B * h + P * (i + 1))
                    d_cols = slice(D * h, D * (h + 1))
                    nc.tensor.matmul_mx(
                        out=bank[:, D * i : D * (i + 1)],
                        lhsT=h3_codes[:, b_cols].bitcast(FP8X4),
                        lhsT_scale=h3_scales[:, b_cols],
                        rhs=w4_codes[:, d_cols].bitcast(FP8X4),
                        rhs_scale=w4_scales[:, d_cols],
                        start=(h == 0),
                        stop=(h == 1),
                    )
            live[("out_bank", e)] = bank

        def add_b4(e):
            nc.vector.tensor_tensor(
                out=out_rows.rearrange("p i (e d) -> p i e d", e=E)[:, :, e, :],
                in0=live[("out_bank", e)][:].rearrange("p (i d) -> p i d", i=2),
                in1=b4_all[:, D * e : D * (e + 1)].unsqueeze(1).to_broadcast([P, 2, D]),
                op=ALU.add,
            )

        def store(first, last):
            cols = slice(D * first, D * (last + 1))
            nc.sync.dma_start(out=out_view[:, :, cols], in_=out_rows[:, :, cols])

        def turn_biases():
            nc.vector.tensor_copy(out=biases_f32[:], in_=biases[:])
            bias_bank = ps_second.tile([P, 2 * D], F32, name="bias_bank", tag="small_bank")
            nc.tensor.transpose(bias_bank[:, 0:P], biases_f32[:], identity[:])
            live["bias_bank"] = bias_bank

        def spread_b4():
            for c in range(2):
                b4_bank = ps_first.tile([P, PACK * D], F32, name="b4_bank", tag="h3_bank")
                for i in range(PACK):
                    col = B3_ROWS + PACK * c + i
                    nc.tensor.transpose(
                        b4_bank[:, D * i : D * (i + 1)],
                        bias_cols[:, col : col + 1].to_broadcast([P, P]),
                        identity[:],
                    )
                live[("b4_bank", c)] = b4_bank

        def copy_b4():
            for c in range(2):
                nc.scalar.copy(out=b4_all[:, PACK * D * c : PACK * D * (c + 1)], in_=live[("b4_bank", c)][:])

        biases = const.tile([P, P], BF16)
        nc.gpsimd.memset(biases[:].bitcast(F32), 0.0)
        identity = const.tile([P, P], F32)
        make_identity(nc, identity[:])
        identity_bf16 = const.tile([P, P], BF16)
        make_identity(nc, identity_bf16[:])
        table_in = const.tile([P, 1], F32)
        nc.vector.memset(table_in[:], 0.0)
        table_out = const.tile([P, 1], F32)
        nc.scalar.activation(out=table_out[:], in_=table_in[:], func=ACT.Silu)

        load_h2(0)
        load_w3(0, 0)
        nc.sync.dma_start(out=biases[0:B3_ROWS, :], in_=b3_rows)
        nc.sync.dma_start(out=biases[B3_ROWS : B3_ROWS + E, :], in_=b4)
        load_w3(0, 1)
        load_environment(1)
        load_environment(2)
        load_environment(3)

        biases_f32 = const.tile([P, P], F32)
        bias_cols = const.tile([P, P], F32)
        b4_all = const.tile([P, E * D], F32)
        out_tile = const.tile([P, 2 * E * D], F32)
        out_rows = out_tile[:].rearrange("p (i x) -> p i x", i=2)

        for s in range(HALVES + 4):
            e, h = s // 2, s % 2
            early = e < EARLY
            if h == 0 and e < E:
                transpose_h2(e)
            if s == 0:
                copy_h2(0)
                quantise_h2(0)
            if 0 <= s - 1 < HALVES:
                quantise_w3(s - 1)
            if s < HALVES:
                regroup_w3(nc.scalar.copy, s, 1 if early and h == 1 else 0)
            if s == 1:
                copy_b4()
            if s in MOVED:
                copy_moved(s)
            if 0 <= s - 3 < HALVES:
                regroup_h3(s - 3)
            if s == 4:
                regroup_w4(0)
            if early and h == 0:
                regroup_w3(nc.vector.tensor_copy, s + 1, 0)
            if s == 0:
                turn_biases()
            if s < HALVES and not (early and h == 1):
                regroup_w3(nc.vector.tensor_copy, s, 1)
            if s == 0:
                nc.vector.tensor_copy(out=bias_cols[:], in_=live["bias_bank"][:, 0:P])
                spread_b4()
            if h == 1 and s + 1 in MOVED:
                move_w3(s + 1)
            if h == 1 and 0 < e < E:
                quantise_h2(e)
            if 0 <= s - 1 < HALVES:
                first_product(s - 1)
            if h == 0 and s + 1 in MOVED:
                move_w3(s + 1)
            if 0 <= s - 2 < HALVES:
                swish(s - 2)
            if h == 0 and 0 < e < E:
                copy_h2(e)
            if h == 0 and 0 <= e - 2 < E:
                quantise_w4(e - 2)
            if 0 <= s - 3 < HALVES:
                quantise_h3(s - 3)
                if h == 0:
                    second_product(e - 2)
            if h == 1 and 1 <= e - 1 < E - 1:
                regroup_w4(e - 1)
            if s == HALVES - 1:
                regroup_w4(E - 1)
            if h == 1 and 0 <= e - 2 < E:
                add_b4(e - 2)
                if e - 2 in STORE_AFTER:
                    store(STORE_AFTER[e - 2], e - 2)
            if s in W3_LOAD_AFTER_STEP:
                load_environment(W3_LOAD_AFTER_STEP[s])
                if W3_LOAD_AFTER_STEP[s] == E - 1:
                    load_w4(E - 1)
